import numpy as np
import ml_dtypes


def mxq(x, axis, fmt="e4m3"):
    dtype, down = {"e4m3": (ml_dtypes.float8_e4m3fn, 7), "e5m2": (ml_dtypes.float8_e5m2, 14)}[fmt]
    v = np.moveaxis(np.asarray(x, np.float32).astype(ml_dtypes.bfloat16).astype(np.float64), axis, -1)
    blocks = v.reshape(v.shape[:-1] + (-1, 32))
    amax = np.abs(blocks).max(-1, keepdims=True)
    byte = np.maximum(np.where(amax > 0, np.frexp(amax)[1] - 1 + 127, 0) - down, 1)
    scale = np.exp2(byte - 127.0)
    codes = (blocks / scale).astype(np.float32).astype(dtype).astype(np.float64)
    return np.moveaxis((codes * scale).reshape(v.shape), -1, axis)


WIDE = False


def mx_kscale(k):
    if not WIDE:
        return np.ones(k)
    levels = np.array([10, -10, 5, -5, 0])
    a = np.random.permutation(np.resize(levels, k // 512 * 4)).reshape(k // 512, 4)
    idx = np.arange(k)
    return np.exp2(a[idx // 512, idx % 128 // 32])


BF16 = ml_dtypes.bfloat16


def bf(x):
    return np.asarray(x, np.float32).astype(BF16)


def f64(x):
    return np.asarray(x).astype(np.float64)


E2M1 = np.array([0.0, 0.5, 1.0, 1.5, 2.0, 3.0, 4.0, 6.0, -0.0, -0.5, -1.0, -1.5, -2.0, -3.0, -4.0, -6.0])


def pack_weight(w, fmt):
    k, n = w.shape
    w = f64(bf(w)).reshape(k // 32, 32, n)
    amax = np.abs(w).max(1)
    if fmt == "e4m3":
        byte = np.frexp(amax)[1] - 1 + 127 - 7
    else:
        mant, ex = np.frexp(amax / 6.0)
        byte = np.where(mant > 0.5, ex, ex - 1) + 127
    byte = np.clip(np.where(amax > 0, byte, 1), 1, 254)
    scaled = (w * np.exp2(127.0 - byte)[:, None, :]).reshape(k, n).astype(np.float32)
    by_word = np.ascontiguousarray(scaled.reshape(k // 512, 128, 4, n).transpose(0, 1, 3, 2))
    if fmt == "e4m3":
        words = by_word.astype(ml_dtypes.float8_e4m3fn).view(np.uint8)
    else:
        c = by_word.astype(ml_dtypes.float4_e2m1fn).view(np.uint8) & 0xF
        words = c[..., 0::2] | (c[..., 1::2] << 4)
    return np.ascontiguousarray(words), np.ascontiguousarray(byte.astype(np.uint8).reshape(k // 512, 16, n))


def unpack_weight(words, scales, fmt):
    g, p, n, _ = words.shape
    if fmt == "e4m3":
        vals = np.ascontiguousarray(words).view(ml_dtypes.float8_e4m3fn).astype(np.float64)
    else:
        nib = np.empty((g, p, n, 4), np.uint8)
        nib[..., 0::2] = words & 0xF
        nib[..., 1::2] = words >> 4
        vals = E2M1[nib]
    vals = vals * np.repeat(np.exp2(scales.astype(np.float64) - 127.0), 8, axis=1)[..., None]
    return vals.transpose(0, 1, 3, 2).reshape(g * 512, n)


BS, L, D, E, H = 1, 128, 4096, 2048, 2
LAMBDA_ATTN = 10.0


def l2norm(x, eps=1e-12):
    n = np.sqrt(np.sum(x * x, axis=-1, keepdims=True))
    return x / np.maximum(n, eps)


def softmax(x, axis):
    e = np.exp(x - x.max(axis=axis, keepdims=True))
    return e / e.sum(axis=axis, keepdims=True)


def setup_inputs():
    s = mx_kscale(D)
    g1 = np.exp2(np.random.uniform(-1.0, 1.0, (BS, 1, L)))
    g2 = np.exp2(np.random.uniform(-1.0, 1.0, (BS, 1, L)))
    img1 = bf(np.random.standard_normal((BS, D, L)) * g1 * s[None, :, None])
    img2 = bf(np.random.standard_normal((BS, D, L)) * g2 * s[None, :, None])
    stack = np.random.standard_normal((H, D, E)) / np.sqrt(D) / s[None, :, None]
    cat = stack.reshape(-1, E)
    words, scales = pack_weight(cat, "e4m3")
    b = bf(np.random.standard_normal((H, E)) * 0.5)
    return {"img1": img1,
            "img2": img2,
            "W_words": words,
            "W_scales": scales,
            "b": b}


def reference(img1, img2, W_words, W_scales, b):
    x1 = np.swapaxes(mxq(f64(img1), 1, "e4m3"), 1, 2)
    x2 = np.swapaxes(mxq(f64(img2), 1, "e4m3"), 1, 2)
    Wf = unpack_weight(W_words, W_scales, "e4m3").reshape(H, D, E).transpose(1, 0, 2).reshape(D, H * E)
    bb = f64(b)[:, None, None, :]
    q1 = (x1 @ Wf).reshape(BS, L, H, E).transpose(2, 0, 1, 3) + bb
    q2 = (x2 @ Wf).reshape(BS, L, H, E).transpose(2, 0, 1, 3) + bb
    n1 = l2norm(q1)
    n2 = l2norm(q2)
    rel = (mxq(n1, 3, "e4m3") @ mxq(n2, 3, "e4m3").transpose(0, 1, 3, 2)) * LAMBDA_ATTN
    row_attn = softmax(rel, 3)
    col_attn = softmax(rel, 2)
    sim12 = row_attn.sum(axis=2)
    sim21 = col_attn.sum(axis=3)
    sim12 = sim12 / (sim12.sum(axis=-1, keepdims=True) + 1e-8)
    sim21 = sim21 / (sim21.sum(axis=-1, keepdims=True) + 1e-8)
    return np.stack([sim21, sim12], axis=0)

@@ -1,0 +1,269 @@
+from contextlib import ExitStack
+
+import concourse.mybir as mybir
+from concourse.masks import make_identity
+
+F32 = mybir.dt.float32
+BF16 = mybir.dt.bfloat16
+I32 = mybir.dt.int32
+U32 = mybir.dt.uint32
+U8 = mybir.dt.uint8
+FP8X4 = mybir.dt.float8_e4m3fn_x4
+ALU = mybir.AluOpType
+ACT = mybir.ActivationFunctionType
+AX = mybir.AxisListType
+
+P = 128
+PACK = 4
+K_PASS = P * PACK
+L = 128
+D = 4096
+E = 2048
+H = 2
+IMAGES = 2
+LAMBDA_ATTN = 10.0
+NORM_FLOOR = 1e-12
+
+D_PASSES = D // K_PASS
+E_PASSES = E // K_PASS
+BANK = 512
+ROUND_COLS = 1024
+ROUND_BANKS = ROUND_COLS // BANK
+ROUNDS = E // ROUND_COLS
+PLANES = 4
+PLANE_SETS = H * D_PASSES // PLANES
+HALF_PASSES = D_PASSES // 2
+SECOND_STAGE_LAG = 4
+
+FLOPS = 2 * IMAGES * H * L * D * E + 2 * H * L * L * E
+
+
+def tile_oaclipv3_w_e_kernel(tc, img1, img2, W_words, W_scales, b, out):
+    nc = tc.nc
+    images = (img1, img2)
+    with ExitStack() as pools:
+        const = pools.enter_context(tc.tile_pool(name="const", bufs=1))
+        weights = pools.enter_context(tc.tile_pool(name="weights", bufs=3))
+        work = pools.enter_context(tc.tile_pool(name="work", bufs=1))
+        small = pools.enter_context(tc.tile_pool(name="small", bufs=2))
+        psum = pools.enter_context(tc.psum_pool(name="psum", bufs=8))
+
+        raw = []
+        for i in range(IMAGES):
+            raw_i = const.tile([P, D_PASSES, PACK, L], BF16, name="raw%d" % i)
+            nc.sync.dma_start(
+                out=raw_i[:], in_=images[i][0].rearrange("(g p t) r -> p g t r", p=P, t=PACK)
+            )
+            raw.append(raw_i)
+
+        w_planes = const.tile([P, PLANE_SETS, E], U8, align_bytes=64)
+        nc.vector.memset(w_planes[:].rearrange("p s n -> p (s n)").bitcast(I32), 0)
+        for s in range(PLANE_SETS):
+            for quadrant in range(4):
+                nc.sync.dma_start(
+                    out=w_planes[32 * quadrant : 32 * quadrant + 4 * PLANES, s, :].bitcast(I32),
+                    in_=W_scales[
+                        PLANES * s : PLANES * (s + 1), 4 * quadrant : 4 * quadrant + 4, :
+                    ].bitcast(I32),
+                )
+
+        def load_round(head, part):
+            w_codes = weights.tile([P, D_PASSES, ROUND_COLS], U32, name="w_codes", align_bytes=64)
+            first_byte = PACK * ROUND_COLS * part
+            for g in range(D_PASSES):
+                nc.sync.dma_start(
+                    out=w_codes[:, g, :].bitcast(I32),
+                    in_=W_words[D_PASSES * head + g]
+                    .rearrange("p n t -> p (n t)")[:, first_byte : first_byte + PACK * ROUND_COLS]
+                    .bitcast(I32),
+                )
+            return w_codes
+
+        rounds = [(head, part) for head in range(H) for part in range(ROUNDS)]
+        loaded = [load_round(head, part) for head, part in rounds[:3]]
+
+        identity = const.tile([P, P], BF16)
+        make_identity(nc, identity[:])
+        ones = const.tile([P, P], BF16)
+        nc.vector.memset(ones[:], 1.0)
+        minus_half = const.tile([P, IMAGES], F32)
+        nc.vector.memset(minus_half[:], -0.5)
+
+        bias_row = const.tile([P, H * E], BF16)
+        nc.vector.memset(bias_row[:], 0.0)
+        nc.scalar.dma_start(out=bias_row[0:1, :], in_=b.rearrange("(o h) e -> o (h e)", o=1))
+        bias_all = const.tile([P, H * E], BF16)
+        for block in range(H * E // BANK):
+            cols = slice(BANK * block, BANK * (block + 1))
+            spread = psum.tile([P, BANK], F32, name="spread", tag="bank")
+            nc.tensor.matmul(spread[:], lhsT=ones[:], rhs=bias_row[:, cols], start=True, stop=True)
+            nc.scalar.copy(out=bias_all[:, cols], in_=spread[:])
+
+        img_codes = const.tile([P, IMAGES, D_PASSES, L], U32, align_bytes=64)
+        img_planes = const.tile([P, IMAGES, D_PASSES, L], U8, align_bytes=64)
+        grouped = [
+            const.tile([P, D_PASSES, L, PACK], BF16, name="grouped%d" % i, align_bytes=64)
+            for i in range(IMAGES)
+        ]
+        first, second = slice(0, HALF_PASSES), slice(HALF_PASSES, D_PASSES)
+        for i in range(IMAGES):
+            nc.vector.tensor_copy(
+                out=grouped[i][:, first], in_=raw[i][:, first].rearrange("p g t r -> p g r t")
+            )
+            nc.scalar.copy(
+                out=grouped[i][:, second], in_=raw[i][:, second].rearrange("p g t r -> p g r t")
+            )
+        for passes in (first, second):
+            for i in range(IMAGES):
+                nc.vector.quantize_mx(
+                    out=img_codes[:, i, passes].rearrange("p g r -> p (g r)").bitcast(FP8X4),
+                    scales=img_planes[:, i, passes].rearrange("p g r -> p (g r)"),
+                    in_=grouped[i][:, passes].rearrange("p g r t -> p (g r t)"),
+                )
+
+        squares = const.tile([P, BANK], BF16)
+        result = const.tile([P, 2, H, L], F32)
+
+        def second_stage(head, biased, square_sums):
+            norm_sq = small.tile([P, IMAGES], F32)
+            nc.vector.tensor_reduce(out=norm_sq[:], in_=square_sums[:], axis=AX.X, op=ALU.add)
+            nc.vector.tensor_scalar_max(
+                out=norm_sq[:], in0=norm_sq[:], scalar1=NORM_FLOOR * NORM_FLOOR
+            )
+            inv_norm = small.tile([P, IMAGES], F32)
+            nc.gpsimd.tensor_tensor(
+                out=inv_norm[:], in0=norm_sq[:], in1=minus_half[:], op=ALU.pow
+            )
+
+            unit_grouped = work.tile([P, E_PASSES, IMAGES, L, PACK], BF16, align_bytes=64)
+            unit_codes = work.tile([P, E_PASSES, IMAGES * L], U32, align_bytes=64)
+            unit_planes = work.tile([P, E_PASSES, IMAGES * L], U8, align_bytes=64)
+            unit = [work.tile([P, E], BF16, name="unit%d" % i) for i in range(IMAGES)]
+            for c in range(E_PASSES):
+                for i in range(IMAGES):
+                    cols = slice(K_PASS * c, K_PASS * (c + 1))
+                    nc.vector.tensor_scalar_mul(
+                        out=unit[i][:, cols], in0=biased[i][:, cols], scalar1=inv_norm[:, i : i + 1]
+                    )
+                    flipped = psum.tile([P, PACK, L], BF16, name="flipped", tag="bank")
+                    for t in range(PACK):
+                        start_col = K_PASS * c + P * t
+                        nc.tensor.transpose(
+                            flipped[:, t, :], unit[i][:, start_col : start_col + P], identity[:]
+                        )
+                    nc.scalar.copy(
+                        out=unit_grouped[:, c, i], in_=flipped[:].rearrange("p t r -> p r t")
+                    )
+                nc.vector.quantize_mx(
+                    out=unit_codes[:, c, :].bitcast(FP8X4),
+                    scales=unit_planes[:, c, :],
+                    in_=unit_grouped[:, c].rearrange("p i r t -> p (i r t)"),
+                )
+
+            scores = psum.tile([P, 2, L], F32, name="scores", tag="bank")
+            for which in range(2):
+                rows = slice(L * (1 - which), L * (2 - which))
+                free = slice(L * which, L * (which + 1))
+                for c in range(E_PASSES):
+                    nc.tensor.matmul_mx(
+                        out=scores[:, which, :],
+                        lhsT=unit_codes[:, c, rows].bitcast(FP8X4),
+                        lhsT_scale=unit_planes[:, c, rows],
+                        rhs=unit_codes[:, c, free].bitcast(FP8X4),
+                        rhs_scale=unit_planes[:, c, free],
+                        start=(c == 0),
+                        stop=(c == E_PASSES - 1),
+                    )
+            row_max = small.tile([P, 2], F32)
+            nc.vector.tensor_reduce(out=row_max[:], in_=scores[:], axis=AX.X, op=ALU.max)
+            shift = small.tile([P, 2], F32)
+            nc.vector.tensor_scalar_mul(out=shift[:], in0=row_max[:], scalar1=-LAMBDA_ATTN)
+            weight = small.tile([P, 2, L], F32)
+            row_sum = small.tile([P, 2], F32)
+            for which in range(2):
+                nc.scalar.activation(
+                    out=weight[:, which, :],
+                    in_=scores[:, which, :],
+                    func=ACT.Exp,
+                    bias=shift[:, which : which + 1],
+                    scale=LAMBDA_ATTN,
+                    accum_out=row_sum[:, which : which + 1],
+                )
+            inv_sum = small.tile([P, 2], F32)
+            nc.vector.reciprocal(out=inv_sum[:], in_=row_sum[:])
+            summed = psum.tile([P, 2, L], F32, name="summed", tag="bank")
+            for which in range(2):
+                nc.tensor.matmul(
+                    summed[:, which, :],
+                    lhsT=inv_sum[:, which : which + 1].to_broadcast([P, P]),
+                    rhs=weight[:, which, :],
+                    start=True,
+                    stop=True,
+                )
+            total = small.tile([P, 2], F32)
+            nc.vector.tensor_reduce(out=total[:], in_=summed[:], axis=AX.X, op=ALU.add)
+            nc.vector.tensor_scalar_add(out=total[:], in0=total[:], scalar1=1e-8)
+            inv_total = small.tile([P, 2], F32)
+            nc.vector.reciprocal(out=inv_total[:], in_=total[:])
+            nc.vector.tensor_tensor(
+                out=result[:, :, head, :],
+                in0=summed[:],
+                in1=inv_total[:].unsqueeze(2).to_broadcast([P, 2, L]),
+                op=ALU.mult,
+            )
+
+        waiting = None
+        for number, (head, part) in enumerate(rounds):
+            w_codes = loaded[number]
+            first_col = ROUND_COLS * part
+            sums = [
+                [psum.tile([P, BANK], F32, name="sums", tag="bank") for c in range(ROUND_BANKS)]
+                for i in range(IMAGES)
+            ]
+            for g in range(D_PASSES):
+                if waiting is not None and g == SECOND_STAGE_LAG:
+                    second_stage(*waiting)
+                    waiting = None
+                s, j = divmod(D_PASSES * head + g, PLANES)
+                for i in range(IMAGES):
+                    for c in range(ROUND_BANKS):
+                        nc.tensor.matmul_mx(
+                            out=sums[i][c][:],
+                            lhsT=img_codes[:, i, g, :].bitcast(FP8X4),
+                            lhsT_scale=img_planes[:, i, g, :],
+                            rhs=w_codes[:, g, BANK * c : BANK * (c + 1)].bitcast(FP8X4),
+                            rhs_scale=w_planes[
+                                4 * j : P, s, first_col + BANK * c : first_col + BANK * (c + 1)
+                            ],
+                            start=(g == 0),
+                            stop=(g == D_PASSES - 1),
+                        )
+            if number + 3 < len(rounds):
+                loaded.append(load_round(*rounds[number + 3]))
+            if part == 0:
+                biased = [work.tile([P, E], F32, name="biased%d" % i) for i in range(IMAGES)]
+                square_sums = small.tile([P, IMAGES, E // BANK], F32)
+            for i in range(IMAGES):
+                for c in range(ROUND_BANKS):
+                    block = ROUND_BANKS * part + c
+                    cols = slice(BANK * block, BANK * (block + 1))
+                    nc.vector.tensor_tensor(
+                        out=biased[i][:, cols],
+                        in0=sums[i][c][:],
+                        in1=bias_all[:, E * head + BANK * block : E * head + BANK * (block + 1)],
+                        op=ALU.add,
+                    )
+                    nc.scalar.activation(
+                        out=squares[:],
+                        in_=biased[i][:, cols],
+                        func=ACT.Square,
+                        accum_out=square_sums[:, i, block : block + 1],
+                    )
+            if part == ROUNDS - 1:
+                waiting = (head, biased, square_sums)
+        second_stage(*waiting)
+
+        nc.sync.dma_start(
+            out=out.flatten_outer_dims().rearrange("(o s) l -> o (s l)", o=1),
+            in_=result[0:1].rearrange("o w h l -> o (w h l)"),
+        )

@@ -33,7 +33,8 @@ ROUNDS = E // ROUND_COLS
 PLANES = 4
 PLANE_SETS = H * D_PASSES // PLANES
 HALF_PASSES = D_PASSES // 2
-SECOND_STAGE_LAG = 4
+FIRST_STEP_AFTER = 6
+STEP_SPACING = 2
 
 FLOPS = 2 * IMAGES * H * L * D * E + 2 * H * L * L * E
 
@@ -46,7 +47,9 @@ def tile_oaclipv3_w_e_kernel(tc, img1, img2, W_words, W_scales, b, out):
         weights = pools.enter_context(tc.tile_pool(name="weights", bufs=3))
         work = pools.enter_context(tc.tile_pool(name="work", bufs=1))
         small = pools.enter_context(tc.tile_pool(name="small", bufs=2))
-        psum = pools.enter_context(tc.psum_pool(name="psum", bufs=8))
+        psum_sums = pools.enter_context(tc.psum_pool(name="psum_sums", bufs=6))
+        psum = pools.enter_context(tc.psum_pool(name="psum", bufs=2))
+        pools.enter_context(tc.manual_schedule())
 
         raw = []
         for i in range(IMAGES):
@@ -95,7 +98,7 @@ def tile_oaclipv3_w_e_kernel(tc, img1, img2, W_words, W_scales, b, out):
         bias_all = const.tile([P, H * E], BF16)
         for block in range(H * E // BANK):
             cols = slice(BANK * block, BANK * (block + 1))
-            spread = psum.tile([P, BANK], F32, name="spread", tag="bank")
+            spread = psum.tile([P, BANK], F32, name="spread", tag="aux")
             nc.tensor.matmul(spread[:], lhsT=ones[:], rhs=bias_row[:, cols], start=True, stop=True)
             nc.scalar.copy(out=bias_all[:, cols], in_=spread[:])
 
@@ -124,7 +127,7 @@ def tile_oaclipv3_w_e_kernel(tc, img1, img2, W_words, W_scales, b, out):
         squares = const.tile([P, BANK], BF16)
         result = const.tile([P, 2, H, L], F32)
 
-        def second_stage(head, biased, square_sums):
+        def second_stage_steps(head, biased, square_sums):
             norm_sq = small.tile([P, IMAGES], F32)
             nc.vector.tensor_reduce(out=norm_sq[:], in_=square_sums[:], axis=AX.X, op=ALU.add)
             nc.vector.tensor_scalar_max(
@@ -134,96 +137,118 @@ def tile_oaclipv3_w_e_kernel(tc, img1, img2, W_words, W_scales, b, out):
             nc.gpsimd.tensor_tensor(
                 out=inv_norm[:], in0=norm_sq[:], in1=minus_half[:], op=ALU.pow
             )
+            unit = [work.tile([P, E], BF16, name="unit%d" % i) for i in range(IMAGES)]
+            for c in range(E_PASSES):
+                cols = slice(K_PASS * c, K_PASS * (c + 1))
+                for i in range(IMAGES):
+                    nc.vector.tensor_scalar_mul(
+                        out=unit[i][:, cols], in0=biased[i][:, cols], scalar1=inv_norm[:, i : i + 1]
+                    )
 
             unit_grouped = work.tile([P, E_PASSES, IMAGES, L, PACK], BF16, align_bytes=64)
             unit_codes = work.tile([P, E_PASSES, IMAGES * L], U32, align_bytes=64)
             unit_planes = work.tile([P, E_PASSES, IMAGES * L], U8, align_bytes=64)
-            unit = [work.tile([P, E], BF16, name="unit%d" % i) for i in range(IMAGES)]
-            for c in range(E_PASSES):
-                for i in range(IMAGES):
-                    cols = slice(K_PASS * c, K_PASS * (c + 1))
-                    nc.vector.tensor_scalar_mul(
-                        out=unit[i][:, cols], in0=biased[i][:, cols], scalar1=inv_norm[:, i : i + 1]
-                    )
-                    flipped = psum.tile([P, PACK, L], BF16, name="flipped", tag="bank")
-                    for t in range(PACK):
-                        start_col = K_PASS * c + P * t
-                        nc.tensor.transpose(
-                            flipped[:, t, :], unit[i][:, start_col : start_col + P], identity[:]
-                        )
+
+            def flip(passes):
+                for c in passes:
+                    flipped = psum.tile([P, IMAGES, PACK, L], BF16, name="flipped", tag="aux")
+                    for i in range(IMAGES):
+                        for t in range(PACK):
+                            start_col = K_PASS * c + P * t
+                            nc.tensor.transpose(
+                                flipped[:, i, t, :],
+                                unit[i][:, start_col : start_col + P],
+                                identity[:],
+                            )
                     nc.scalar.copy(
-                        out=unit_grouped[:, c, i], in_=flipped[:].rearrange("p t r -> p r t")
+                        out=unit_grouped[:, c], in_=flipped[:].rearrange("p i t r -> p i r t")
                     )
-                nc.vector.quantize_mx(
-                    out=unit_codes[:, c, :].bitcast(FP8X4),
-                    scales=unit_planes[:, c, :],
-                    in_=unit_grouped[:, c].rearrange("p i r t -> p (i r t)"),
-                )
 
-            scores = psum.tile([P, 2, L], F32, name="scores", tag="bank")
-            for which in range(2):
-                rows = slice(L * (1 - which), L * (2 - which))
-                free = slice(L * which, L * (which + 1))
-                for c in range(E_PASSES):
-                    nc.tensor.matmul_mx(
-                        out=scores[:, which, :],
-                        lhsT=unit_codes[:, c, rows].bitcast(FP8X4),
-                        lhsT_scale=unit_planes[:, c, rows],
-                        rhs=unit_codes[:, c, free].bitcast(FP8X4),
-                        rhs_scale=unit_planes[:, c, free],
-                        start=(c == 0),
-                        stop=(c == E_PASSES - 1),
+            def quantise(passes):
+                for c in passes:
+                    nc.vector.quantize_mx(
+                        out=unit_codes[:, c, :].bitcast(FP8X4),
+                        scales=unit_planes[:, c, :],
+                        in_=unit_grouped[:, c].rearrange("p i r t -> p (i r t)"),
                     )
-            row_max = small.tile([P, 2], F32)
-            nc.vector.tensor_reduce(out=row_max[:], in_=scores[:], axis=AX.X, op=ALU.max)
-            shift = small.tile([P, 2], F32)
-            nc.vector.tensor_scalar_mul(out=shift[:], in0=row_max[:], scalar1=-LAMBDA_ATTN)
+
             weight = small.tile([P, 2, L], F32)
-            row_sum = small.tile([P, 2], F32)
-            for which in range(2):
-                nc.scalar.activation(
-                    out=weight[:, which, :],
-                    in_=scores[:, which, :],
-                    func=ACT.Exp,
-                    bias=shift[:, which : which + 1],
-                    scale=LAMBDA_ATTN,
-                    accum_out=row_sum[:, which : which + 1],
-                )
             inv_sum = small.tile([P, 2], F32)
-            nc.vector.reciprocal(out=inv_sum[:], in_=row_sum[:])
-            summed = psum.tile([P, 2, L], F32, name="summed", tag="bank")
-            for which in range(2):
-                nc.tensor.matmul(
-                    summed[:, which, :],
-                    lhsT=inv_sum[:, which : which + 1].to_broadcast([P, P]),
-                    rhs=weight[:, which, :],
-                    start=True,
-                    stop=True,
-                )
-            total = small.tile([P, 2], F32)
-            nc.vector.tensor_reduce(out=total[:], in_=summed[:], axis=AX.X, op=ALU.add)
-            nc.vector.tensor_scalar_add(out=total[:], in0=total[:], scalar1=1e-8)
-            inv_total = small.tile([P, 2], F32)
-            nc.vector.reciprocal(out=inv_total[:], in_=total[:])
-            nc.vector.tensor_tensor(
-                out=result[:, :, head, :],
-                in0=summed[:],
-                in1=inv_total[:].unsqueeze(2).to_broadcast([P, 2, L]),
-                op=ALU.mult,
-            )
 
-        waiting = None
+            def attend():
+                scores = psum.tile([P, 2, L], F32, name="scores", tag="aux")
+                for which in range(2):
+                    rows = slice(L * (1 - which), L * (2 - which))
+                    free = slice(L * which, L * (which + 1))
+                    for c in range(E_PASSES):
+                        nc.tensor.matmul_mx(
+                            out=scores[:, which, :],
+                            lhsT=unit_codes[:, c, rows].bitcast(FP8X4),
+                            lhsT_scale=unit_planes[:, c, rows],
+                            rhs=unit_codes[:, c, free].bitcast(FP8X4),
+                            rhs_scale=unit_planes[:, c, free],
+                            start=(c == 0),
+                            stop=(c == E_PASSES - 1),
+                        )
+                row_max = small.tile([P, 2], F32)
+                nc.vector.tensor_reduce(out=row_max[:], in_=scores[:], axis=AX.X, op=ALU.max)
+                shift = small.tile([P, 2], F32)
+                nc.vector.tensor_scalar_mul(out=shift[:], in0=row_max[:], scalar1=-LAMBDA_ATTN)
+                row_sum = small.tile([P, 2], F32)
+                for which in range(2):
+                    nc.scalar.activation(
+                        out=weight[:, which, :],
+                        in_=scores[:, which, :],
+                        func=ACT.Exp,
+                        bias=shift[:, which : which + 1],
+                        scale=LAMBDA_ATTN,
+                        accum_out=row_sum[:, which : which + 1],
+                    )
+                nc.vector.reciprocal(out=inv_sum[:], in_=row_sum[:])
+
+            def add_up():
+                summed = psum.tile([P, 2, L], F32, name="summed", tag="aux")
+                for which in range(2):
+                    nc.tensor.matmul(
+                        summed[:, which, :],
+                        lhsT=inv_sum[:, which : which + 1].to_broadcast([P, P]),
+                        rhs=weight[:, which, :],
+                        start=True,
+                        stop=True,
+                    )
+                total = small.tile([P, 2], F32)
+                nc.vector.tensor_reduce(out=total[:], in_=summed[:], axis=AX.X, op=ALU.add)
+                nc.vector.tensor_scalar_add(out=total[:], in0=total[:], scalar1=1e-8)
+                inv_total = small.tile([P, 2], F32)
+                nc.vector.reciprocal(out=inv_total[:], in_=total[:])
+                nc.vector.tensor_tensor(
+                    out=result[:, :, head, :],
+                    in0=summed[:],
+                    in1=inv_total[:].unsqueeze(2).to_broadcast([P, 2, L]),
+                    op=ALU.mult,
+                )
+
+            early, late = range(0, E_PASSES // 2), range(E_PASSES // 2, E_PASSES)
+
+            def step_two():
+                quantise(early)
+                flip(late)
+
+            def step_three():
+                quantise(late)
+                attend()
+
+            return [lambda: flip(early), step_two, step_three, add_up]
+
+        steps = []
         for number, (head, part) in enumerate(rounds):
             w_codes = loaded[number]
             first_col = ROUND_COLS * part
             sums = [
-                [psum.tile([P, BANK], F32, name="sums", tag="bank") for c in range(ROUND_BANKS)]
+                [psum_sums.tile([P, BANK], F32, name="sums") for c in range(ROUND_BANKS)]
                 for i in range(IMAGES)
             ]
             for g in range(D_PASSES):
-                if waiting is not None and g == SECOND_STAGE_LAG:
-                    second_stage(*waiting)
-                    waiting = None
                 s, j = divmod(D_PASSES * head + g, PLANES)
                 for i in range(IMAGES):
                     for c in range(ROUND_BANKS):
@@ -238,6 +263,9 @@ def tile_oaclipv3_w_e_kernel(tc, img1, img2, W_words, W_scales, b, out):
                             start=(g == 0),
                             stop=(g == D_PASSES - 1),
                         )
+                done = D_PASSES * part + g - FIRST_STEP_AFTER
+                if steps and done >= 0 and done % STEP_SPACING == 0:
+                    steps.pop(0)()
             if number + 3 < len(rounds):
                 loaded.append(load_round(*rounds[number + 3]))
             if part == 0:
@@ -260,8 +288,9 @@ def tile_oaclipv3_w_e_kernel(tc, img1, img2, W_words, W_scales, b, out):
                         accum_out=square_sums[:, i, block : block + 1],
                     )
             if part == ROUNDS - 1:
-                waiting = (head, biased, square_sums)
-        second_stage(*waiting)
+                steps = second_stage_steps(head, biased, square_sums)
+        for step in steps:
+            step()
 
         nc.sync.dma_start(
             out=out.flatten_outer_dims().rearrange("(o s) l -> o (s l)", o=1),

@@ -28,13 +28,12 @@ D_PASSES = D // K_PASS
 E_PASSES = E // K_PASS
 BANK = 512
 ROUND_COLS = 1024
-ROUND_BANKS = ROUND_COLS // BANK
-ROUNDS = E // ROUND_COLS
 PLANES = 4
 PLANE_SETS = H * D_PASSES // PLANES
 HALF_PASSES = D_PASSES // 2
-FIRST_STEP_AFTER = 6
-STEP_SPACING = 2
+W_BUFS = 3
+FIRST_STEP_AT = 7 * ROUND_COLS
+STEP_SPACING = 2 * ROUND_COLS
 
 FLOPS = 2 * IMAGES * H * L * D * E + 2 * H * L * L * E
 
@@ -44,24 +43,20 @@ def tile_oaclipv3_w_e_kernel(tc, img1, img2, W_words, W_scales, b, out):
     images = (img1, img2)
     with ExitStack() as pools:
         const = pools.enter_context(tc.tile_pool(name="const", bufs=1))
-        weights = pools.enter_context(tc.tile_pool(name="weights", bufs=3))
+        weights = pools.enter_context(tc.tile_pool(name="weights", bufs=W_BUFS))
         work = pools.enter_context(tc.tile_pool(name="work", bufs=1))
         small = pools.enter_context(tc.tile_pool(name="small", bufs=2))
         psum_sums = pools.enter_context(tc.psum_pool(name="psum_sums", bufs=6))
         psum = pools.enter_context(tc.psum_pool(name="psum", bufs=2))
         pools.enter_context(tc.manual_schedule())
 
-        raw = []
-        for i in range(IMAGES):
-            raw_i = const.tile([P, D_PASSES, PACK, L], BF16, name="raw%d" % i)
-            nc.sync.dma_start(
-                out=raw_i[:], in_=images[i][0].rearrange("(g p t) r -> p g t r", p=P, t=PACK)
-            )
-            raw.append(raw_i)
-
         w_planes = const.tile([P, PLANE_SETS, E], U8, align_bytes=64)
         nc.vector.memset(w_planes[:].rearrange("p s n -> p (s n)").bitcast(I32), 0)
-        for s in range(PLANE_SETS):
+        bias_row = const.tile([P, H * E], BF16)
+        nc.vector.memset(bias_row[:].bitcast(I32), 0)
+        nc.gpsimd.dma_start(out=bias_row[0:1, :], in_=b.rearrange("(o h) e -> o (h e)", o=1))
+
+        def load_plane_set(s):
             for quadrant in range(4):
                 nc.sync.dma_start(
                     out=w_planes[32 * quadrant : 32 * quadrant + 4 * PLANES, s, :].bitcast(I32),
@@ -70,20 +65,35 @@ def tile_oaclipv3_w_e_kernel(tc, img1, img2, W_words, W_scales, b, out):
                     ].bitcast(I32),
                 )
 
-        def load_round(head, part):
-            w_codes = weights.tile([P, D_PASSES, ROUND_COLS], U32, name="w_codes", align_bytes=64)
-            first_byte = PACK * ROUND_COLS * part
+        load_plane_set(0)
+        first, second = slice(0, HALF_PASSES), slice(HALF_PASSES, D_PASSES)
+        raw = [const.tile([P, D_PASSES, PACK, L], BF16, name="raw%d" % i) for i in range(IMAGES)]
+        for passes in (first, second):
+            for i in range(IMAGES):
+                nc.scalar.dma_start(
+                    out=raw[i][:, passes],
+                    in_=images[i][0].rearrange("(g p t) r -> p g t r", p=P, t=PACK)[:, passes],
+                )
+        for s in range(1, PLANE_SETS):
+            load_plane_set(s)
+
+        def load_round(head, first_col, cols):
+            w_codes = weights.tile([P, D_PASSES, cols], U32, name="w_codes", align_bytes=64)
             for g in range(D_PASSES):
                 nc.sync.dma_start(
                     out=w_codes[:, g, :].bitcast(I32),
                     in_=W_words[D_PASSES * head + g]
-                    .rearrange("p n t -> p (n t)")[:, first_byte : first_byte + PACK * ROUND_COLS]
+                    .rearrange("p n t -> p (n t)")[:, PACK * first_col : PACK * (first_col + cols)]
                     .bitcast(I32),
                 )
             return w_codes
 
-        rounds = [(head, part) for head in range(H) for part in range(ROUNDS)]
-        loaded = [load_round(head, part) for head, part in rounds[:3]]
+        rounds = [
+            (head, first_col, ROUND_COLS) for head in range(H) for first_col in range(0, E, ROUND_COLS)
+        ]
+        head, first_col, cols = rounds.pop()
+        rounds += [(head, first_col, cols // 2), (head, first_col + cols // 2, cols // 2)]
+        loaded = [load_round(*rounds[number]) for number in range(W_BUFS)]
 
         identity = const.tile([P, P], BF16)
         make_identity(nc, identity[:])
@@ -92,15 +102,14 @@ def tile_oaclipv3_w_e_kernel(tc, img1, img2, W_words, W_scales, b, out):
         minus_half = const.tile([P, IMAGES], F32)
         nc.vector.memset(minus_half[:], -0.5)
 
-        bias_row = const.tile([P, H * E], BF16)
-        nc.vector.memset(bias_row[:], 0.0)
-        nc.scalar.dma_start(out=bias_row[0:1, :], in_=b.rearrange("(o h) e -> o (h e)", o=1))
         bias_all = const.tile([P, H * E], BF16)
         for block in range(H * E // BANK):
-            cols = slice(BANK * block, BANK * (block + 1))
-            spread = psum.tile([P, BANK], F32, name="spread", tag="aux")
-            nc.tensor.matmul(spread[:], lhsT=ones[:], rhs=bias_row[:, cols], start=True, stop=True)
-            nc.scalar.copy(out=bias_all[:, cols], in_=spread[:])
+            block_cols = slice(BANK * block, BANK * (block + 1))
+            spread = psum_sums.tile([P, BANK], F32, name="sums")
+            nc.tensor.matmul(
+                spread[:], lhsT=ones[:], rhs=bias_row[:, block_cols], start=True, stop=True
+            )
+            nc.scalar.copy(out=bias_all[:, block_cols], in_=spread[:])
 
         img_codes = const.tile([P, IMAGES, D_PASSES, L], U32, align_bytes=64)
         img_planes = const.tile([P, IMAGES, D_PASSES, L], U8, align_bytes=64)
@@ -108,15 +117,11 @@ def tile_oaclipv3_w_e_kernel(tc, img1, img2, W_words, W_scales, b, out):
             const.tile([P, D_PASSES, L, PACK], BF16, name="grouped%d" % i, align_bytes=64)
             for i in range(IMAGES)
         ]
-        first, second = slice(0, HALF_PASSES), slice(HALF_PASSES, D_PASSES)
-        for i in range(IMAGES):
-            nc.vector.tensor_copy(
-                out=grouped[i][:, first], in_=raw[i][:, first].rearrange("p g t r -> p g r t")
-            )
-            nc.scalar.copy(
-                out=grouped[i][:, second], in_=raw[i][:, second].rearrange("p g t r -> p g r t")
-            )
         for passes in (first, second):
+            for i in range(IMAGES):
+                nc.vector.tensor_copy(
+                    out=grouped[i][:, passes], in_=raw[i][:, passes].rearrange("p g t r -> p g r t")
+                )
             for i in range(IMAGES):
                 nc.vector.quantize_mx(
                     out=img_codes[:, i, passes].rearrange("p g r -> p (g r)").bitcast(FP8X4),
@@ -241,17 +246,20 @@ def tile_oaclipv3_w_e_kernel(tc, img1, img2, W_words, W_scales, b, out):
             return [lambda: flip(early), step_two, step_three, add_up]
 
         steps = []
-        for number, (head, part) in enumerate(rounds):
+        for number, (head, first_col, cols) in enumerate(rounds):
             w_codes = loaded[number]
-            first_col = ROUND_COLS * part
+            banks = cols // BANK
+            if first_col == 0:
+                written = 0
+                next_step_at = FIRST_STEP_AT
             sums = [
-                [psum_sums.tile([P, BANK], F32, name="sums") for c in range(ROUND_BANKS)]
+                [psum_sums.tile([P, BANK], F32, name="sums") for c in range(banks)]
                 for i in range(IMAGES)
             ]
             for g in range(D_PASSES):
                 s, j = divmod(D_PASSES * head + g, PLANES)
                 for i in range(IMAGES):
-                    for c in range(ROUND_BANKS):
+                    for c in range(banks):
                         nc.tensor.matmul_mx(
                             out=sums[i][c][:],
                             lhsT=img_codes[:, i, g, :].bitcast(FP8X4),
@@ -263,31 +271,32 @@ def tile_oaclipv3_w_e_kernel(tc, img1, img2, W_words, W_scales, b, out):
                             start=(g == 0),
                             stop=(g == D_PASSES - 1),
                         )
-                done = D_PASSES * part + g - FIRST_STEP_AFTER
-                if steps and done >= 0 and done % STEP_SPACING == 0:
+                written += cols
+                if steps and written >= next_step_at and g < D_PASSES - 1:
                     steps.pop(0)()
-            if number + 3 < len(rounds):
-                loaded.append(load_round(*rounds[number + 3]))
-            if part == 0:
+                    next_step_at += STEP_SPACING
+            if number + W_BUFS < len(rounds):
+                loaded.append(load_round(*rounds[number + W_BUFS]))
+            if first_col == 0:
                 biased = [work.tile([P, E], F32, name="biased%d" % i) for i in range(IMAGES)]
                 square_sums = small.tile([P, IMAGES, E // BANK], F32)
             for i in range(IMAGES):
-                for c in range(ROUND_BANKS):
-                    block = ROUND_BANKS * part + c
-                    cols = slice(BANK * block, BANK * (block + 1))
+                for c in range(banks):
+                    block = first_col // BANK + c
+                    block_cols = slice(BANK * block, BANK * (block + 1))
                     nc.vector.tensor_tensor(
-                        out=biased[i][:, cols],
+                        out=biased[i][:, block_cols],
                         in0=sums[i][c][:],
                         in1=bias_all[:, E * head + BANK * block : E * head + BANK * (block + 1)],
                         op=ALU.add,
                     )
                     nc.scalar.activation(
                         out=squares[:],
-                        in_=biased[i][:, cols],
+                        in_=biased[i][:, block_cols],
                         func=ACT.Square,
                         accum_out=square_sums[:, i, block : block + 1],
                     )
-            if part == ROUNDS - 1:
+            if first_col + cols == E:
                 steps = second_stage_steps(head, biased, square_sums)
         for step in steps:
             step()

@@ -30,7 +30,7 @@ BANK = 512
 ROUND_COLS = 1024
 PLANES = 4
 PLANE_SETS = H * D_PASSES // PLANES
-HALF_PASSES = D_PASSES // 2
+IMAGE_CHUNKS = (slice(0, 1), slice(1, 2), slice(2, 4), slice(4, 6), slice(6, 8))
 W_BUFS = 3
 FIRST_STEP_AT = 7 * ROUND_COLS
 STEP_SPACING = 2 * ROUND_COLS
@@ -50,42 +50,55 @@ def tile_oaclipv3_w_e_kernel(tc, img1, img2, W_words, W_scales, b, out):
         psum = pools.enter_context(tc.psum_pool(name="psum", bufs=2))
         pools.enter_context(tc.manual_schedule())
 
-        w_planes = const.tile([P, PLANE_SETS, E], U8, align_bytes=64)
-        nc.vector.memset(w_planes[:].rearrange("p s n -> p (s n)").bitcast(I32), 0)
-        bias_row = const.tile([P, H * E], BF16)
-        nc.vector.memset(bias_row[:].bitcast(I32), 0)
-        nc.gpsimd.dma_start(out=bias_row[0:1, :], in_=b.rearrange("(o h) e -> o (h e)", o=1))
+        w_planes = [
+            const.tile([P, E], U8, name="w_planes%d" % s, align_bytes=64) for s in range(PLANE_SETS)
+        ]
+        nc.vector.memset(w_planes[0][:].bitcast(I32), 0)
+        bias_rows = const.tile([P, BANK], BF16)
+        nc.vector.memset(bias_rows[:].bitcast(I32), 0)
+        minus_half = const.tile([P, 1], F32)
+        nc.vector.memset(minus_half[:], -0.5)
+        for s in range(1, PLANE_SETS):
+            nc.vector.memset(w_planes[s][:].bitcast(I32), 0)
+        identity = const.tile([P, P], BF16)
+        make_identity(nc, identity[:])
+        identity_words = const.tile([P, P], F32)
+        make_identity(nc, identity_words[:])
 
         def load_plane_set(s):
             for quadrant in range(4):
                 nc.sync.dma_start(
-                    out=w_planes[32 * quadrant : 32 * quadrant + 4 * PLANES, s, :].bitcast(I32),
+                    out=w_planes[s][32 * quadrant : 32 * quadrant + 4 * PLANES, :].bitcast(I32),
                     in_=W_scales[
                         PLANES * s : PLANES * (s + 1), 4 * quadrant : 4 * quadrant + 4, :
                     ].bitcast(I32),
                 )
 
-        load_plane_set(0)
-        first, second = slice(0, HALF_PASSES), slice(HALF_PASSES, D_PASSES)
         raw = [const.tile([P, D_PASSES, PACK, L], BF16, name="raw%d" % i) for i in range(IMAGES)]
-        for passes in (first, second):
+
+        def load_images(queue, passes):
             for i in range(IMAGES):
-                nc.scalar.dma_start(
+                queue.dma_start(
                     out=raw[i][:, passes],
                     in_=images[i][0].rearrange("(g p t) r -> p g t r", p=P, t=PACK)[:, passes],
                 )
-        for s in range(1, PLANE_SETS):
-            load_plane_set(s)
 
-        def load_round(head, first_col, cols):
+        def load_pass(w_codes, head, g, first_col, cols):
+            nc.sync.dma_start(
+                out=w_codes[:, g, :].bitcast(I32),
+                in_=W_words[D_PASSES * head + g]
+                .rearrange("p n t -> p (n t)")[:, PACK * first_col : PACK * (first_col + cols)]
+                .bitcast(I32),
+            )
+
+        def load_round(head, first_col, cols, image_chunks={}, plane_sets={}):
             w_codes = weights.tile([P, D_PASSES, cols], U32, name="w_codes", align_bytes=64)
             for g in range(D_PASSES):
-                nc.sync.dma_start(
-                    out=w_codes[:, g, :].bitcast(I32),
-                    in_=W_words[D_PASSES * head + g]
-                    .rearrange("p n t -> p (n t)")[:, PACK * first_col : PACK * (first_col + cols)]
-                    .bitcast(I32),
-                )
+                if g in plane_sets:
+                    load_plane_set(plane_sets[g])
+                if g in image_chunks:
+                    load_images(nc.sync, image_chunks[g])
+                load_pass(w_codes, head, g, first_col, cols)
             return w_codes
 
         rounds = [
@@ -93,23 +106,33 @@ def tile_oaclipv3_w_e_kernel(tc, img1, img2, W_words, W_scales, b, out):
         ]
         head, first_col, cols = rounds.pop()
         rounds += [(head, first_col, cols // 2), (head, first_col + cols // 2, cols // 2)]
-        loaded = [load_round(*rounds[number]) for number in range(W_BUFS)]
 
-        identity = const.tile([P, P], BF16)
-        make_identity(nc, identity[:])
-        ones = const.tile([P, P], BF16)
-        nc.vector.memset(ones[:], 1.0)
-        minus_half = const.tile([P, IMAGES], F32)
-        nc.vector.memset(minus_half[:], -0.5)
+        load_images(nc.scalar, IMAGE_CHUNKS[0])
+        nc.scalar.dma_start(
+            out=bias_rows[: H * E // BANK, :], in_=b.rearrange("h (c n) -> (h c) n", n=BANK)
+        )
+        load_plane_set(0)
+        loaded = [
+            load_round(
+                *rounds[0],
+                image_chunks={passes.start: passes for passes in IMAGE_CHUNKS[1:]},
+                plane_sets={PLANES: 1},
+            ),
+            load_round(*rounds[1], plane_sets={2: 2, 6: 3}),
+            load_round(*rounds[2]),
+        ]
 
         bias_all = const.tile([P, H * E], BF16)
         for block in range(H * E // BANK):
-            block_cols = slice(BANK * block, BANK * (block + 1))
             spread = psum_sums.tile([P, BANK], F32, name="sums")
             nc.tensor.matmul(
-                spread[:], lhsT=ones[:], rhs=bias_row[:, block_cols], start=True, stop=True
+                spread[:],
+                lhsT=identity[:, block : block + 1].to_broadcast([P, P]),
+                rhs=bias_rows[:],
+                start=True,
+                stop=True,
             )
-            nc.scalar.copy(out=bias_all[:, block_cols], in_=spread[:])
+            nc.scalar.copy(out=bias_all[:, BANK * block : BANK * (block + 1)], in_=spread[:])
 
         img_codes = const.tile([P, IMAGES, D_PASSES, L], U32, align_bytes=64)
         img_planes = const.tile([P, IMAGES, D_PASSES, L], U8, align_bytes=64)
@@ -117,7 +140,7 @@ def tile_oaclipv3_w_e_kernel(tc, img1, img2, W_words, W_scales, b, out):
             const.tile([P, D_PASSES, L, PACK], BF16, name="grouped%d" % i, align_bytes=64)
             for i in range(IMAGES)
         ]
-        for passes in (first, second):
+        for passes in IMAGE_CHUNKS:
             for i in range(IMAGES):
                 nc.vector.tensor_copy(
                     out=grouped[i][:, passes], in_=raw[i][:, passes].rearrange("p g t r -> p g r t")
@@ -132,118 +155,187 @@ def tile_oaclipv3_w_e_kernel(tc, img1, img2, W_words, W_scales, b, out):
         squares = const.tile([P, BANK], BF16)
         result = const.tile([P, 2, H, L], F32)
 
-        def second_stage_steps(head, biased, square_sums):
-            norm_sq = small.tile([P, IMAGES], F32)
-            nc.vector.tensor_reduce(out=norm_sq[:], in_=square_sums[:], axis=AX.X, op=ALU.add)
-            nc.vector.tensor_scalar_max(
-                out=norm_sq[:], in0=norm_sq[:], scalar1=NORM_FLOOR * NORM_FLOOR
-            )
+        def second_stage(head, biased, square_sums, bank_tile):
             inv_norm = small.tile([P, IMAGES], F32)
-            nc.gpsimd.tensor_tensor(
-                out=inv_norm[:], in0=norm_sq[:], in1=minus_half[:], op=ALU.pow
-            )
             unit = [work.tile([P, E], BF16, name="unit%d" % i) for i in range(IMAGES)]
-            for c in range(E_PASSES):
-                cols = slice(K_PASS * c, K_PASS * (c + 1))
+            grouped_words = work.tile([P, E_PASSES, IMAGES, L, PACK // 2], F32, align_bytes=64)
+            unit_codes = work.tile([P, E_PASSES, IMAGES * L], U32, align_bytes=64)
+            unit_planes = work.tile([P, E_PASSES, IMAGES * L], U8, align_bytes=64)
+
+            def norms():
+                rest = small.tile([P, IMAGES], F32)
+                nc.vector.tensor_reduce(
+                    out=rest[:], in_=square_sums[:, :, : E // BANK - 1], axis=AX.X, op=ALU.add
+                )
+                norm_sq = small.tile([P, IMAGES], F32)
                 for i in range(IMAGES):
+                    nc.vector.tensor_scalar(
+                        out=norm_sq[:, i : i + 1],
+                        in0=square_sums[:, i, E // BANK - 1 :],
+                        scalar1=rest[:, i : i + 1],
+                        scalar2=NORM_FLOOR * NORM_FLOOR,
+                        op0=ALU.add,
+                        op1=ALU.max,
+                    )
+                    nc.gpsimd.tensor_tensor(
+                        out=inv_norm[:, i : i + 1],
+                        in0=norm_sq[:, i : i + 1],
+                        in1=minus_half[:],
+                        op=ALU.pow,
+                    )
+
+            def normalise(i, c, on_scalar=False):
+                cols = slice(K_PASS * c, K_PASS * (c + 1))
+                if on_scalar:
+                    nc.scalar.activation(
+                        out=unit[i][:, cols],
+                        in_=biased[i][:, cols],
+                        func=ACT.Copy,
+                        scale=inv_norm[:, i : i + 1],
+                    )
+                else:
                     nc.vector.tensor_scalar_mul(
                         out=unit[i][:, cols], in0=biased[i][:, cols], scalar1=inv_norm[:, i : i + 1]
                     )
 
-            unit_grouped = work.tile([P, E_PASSES, IMAGES, L, PACK], BF16, align_bytes=64)
-            unit_codes = work.tile([P, E_PASSES, IMAGES * L], U32, align_bytes=64)
-            unit_planes = work.tile([P, E_PASSES, IMAGES * L], U8, align_bytes=64)
+            def flip(c):
+                flipped = bank_tile()
+                flipped = flipped[:].rearrange("p (i u r) -> p i u r", i=IMAGES, u=PACK // 2)
+                for i in range(IMAGES):
+                    words = unit[i][:, K_PASS * c : K_PASS * (c + 1)].bitcast(F32)
+                    for u in range(PACK // 2):
+                        nc.tensor.transpose(
+                            flipped[:, i, u, :], words[:, P * u : P * (u + 1)], identity_words[:]
+                        )
+                nc.scalar.copy(
+                    out=grouped_words[:, c], in_=flipped.rearrange("p i u r -> p i r u")
+                )
 
-            def flip(passes):
-                for c in passes:
-                    flipped = psum.tile([P, IMAGES, PACK, L], BF16, name="flipped", tag="aux")
-                    for i in range(IMAGES):
-                        for t in range(PACK):
-                            start_col = K_PASS * c + P * t
-                            nc.tensor.transpose(
-                                flipped[:, i, t, :],
-                                unit[i][:, start_col : start_col + P],
-                                identity[:],
-                            )
-                    nc.scalar.copy(
-                        out=unit_grouped[:, c], in_=flipped[:].rearrange("p i t r -> p i r t")
-                    )
+            def quantise(c):
+                nc.vector.quantize_mx(
+                    out=unit_codes[:, c, :].bitcast(FP8X4),
+                    scales=unit_planes[:, c, :],
+                    in_=grouped_words[:, c].rearrange("p i r u -> p (i r u)").bitcast(BF16),
+                )
 
-            def quantise(passes):
-                for c in passes:
-                    nc.vector.quantize_mx(
-                        out=unit_codes[:, c, :].bitcast(FP8X4),
-                        scales=unit_planes[:, c, :],
-                        in_=unit_grouped[:, c].rearrange("p i r t -> p (i r t)"),
+            scores = []
+
+            def score(c):
+                if c == 0:
+                    for which in range(2):
+                        scores.append(psum.tile([P, BANK], F32, name="scores", tag="aux"))
+                for which in range(2):
+                    rows = slice(L * (1 - which), L * (2 - which))
+                    free = slice(L * which, L * (which + 1))
+                    nc.tensor.matmul_mx(
+                        out=scores[which][:, :L],
+                        lhsT=unit_codes[:, c, rows].bitcast(FP8X4),
+                        lhsT_scale=unit_planes[:, c, rows],
+                        rhs=unit_codes[:, c, free].bitcast(FP8X4),
+                        rhs_scale=unit_planes[:, c, free],
+                        start=(c == 0),
+                        stop=(c == E_PASSES - 1),
                     )
 
             weight = small.tile([P, 2, L], F32)
             inv_sum = small.tile([P, 2], F32)
 
-            def attend():
-                scores = psum.tile([P, 2, L], F32, name="scores", tag="aux")
-                for which in range(2):
-                    rows = slice(L * (1 - which), L * (2 - which))
-                    free = slice(L * which, L * (which + 1))
-                    for c in range(E_PASSES):
-                        nc.tensor.matmul_mx(
-                            out=scores[:, which, :],
-                            lhsT=unit_codes[:, c, rows].bitcast(FP8X4),
-                            lhsT_scale=unit_planes[:, c, rows],
-                            rhs=unit_codes[:, c, free].bitcast(FP8X4),
-                            rhs_scale=unit_planes[:, c, free],
-                            start=(c == 0),
-                            stop=(c == E_PASSES - 1),
-                        )
-                row_max = small.tile([P, 2], F32)
-                nc.vector.tensor_reduce(out=row_max[:], in_=scores[:], axis=AX.X, op=ALU.max)
+            def soften():
                 shift = small.tile([P, 2], F32)
-                nc.vector.tensor_scalar_mul(out=shift[:], in0=row_max[:], scalar1=-LAMBDA_ATTN)
                 row_sum = small.tile([P, 2], F32)
+                for which in range(2):
+                    negated = small.tile([P, L], F32)
+                    nc.vector.tensor_scalar(
+                        out=negated[:],
+                        in0=scores[which][:, :L],
+                        scalar1=-LAMBDA_ATTN,
+                        scalar2=None,
+                        op0=ALU.mult,
+                        op1=ALU.min,
+                        accum_out=shift[:, which : which + 1],
+                    )
                 for which in range(2):
                     nc.scalar.activation(
                         out=weight[:, which, :],
-                        in_=scores[:, which, :],
+                        in_=scores[which][:, :L],
                         func=ACT.Exp,
                         bias=shift[:, which : which + 1],
                         scale=LAMBDA_ATTN,
                         accum_out=row_sum[:, which : which + 1],
                     )
-                nc.vector.reciprocal(out=inv_sum[:], in_=row_sum[:])
+                for which in range(2):
+                    nc.vector.reciprocal(
+                        out=inv_sum[:, which : which + 1], in_=row_sum[:, which : which + 1]
+                    )
 
             def add_up():
-                summed = psum.tile([P, 2, L], F32, name="summed", tag="aux")
+                summed = bank_tile()
                 for which in range(2):
                     nc.tensor.matmul(
-                        summed[:, which, :],
+                        summed[:, L * which : L * (which + 1)],
                         lhsT=inv_sum[:, which : which + 1].to_broadcast([P, P]),
                         rhs=weight[:, which, :],
                         start=True,
                         stop=True,
                     )
-                total = small.tile([P, 2], F32)
-                nc.vector.tensor_reduce(out=total[:], in_=summed[:], axis=AX.X, op=ALU.add)
-                nc.vector.tensor_scalar_add(out=total[:], in0=total[:], scalar1=1e-8)
-                inv_total = small.tile([P, 2], F32)
-                nc.vector.reciprocal(out=inv_total[:], in_=total[:])
-                nc.vector.tensor_tensor(
+                nc.vector.tensor_scalar_mul(
                     out=result[:, :, head, :],
-                    in0=summed[:],
-                    in1=inv_total[:].unsqueeze(2).to_broadcast([P, 2, L]),
-                    op=ALU.mult,
+                    in0=summed[:, : 2 * L].rearrange("p (w l) -> p w l", w=2),
+                    scalar1=1.0 / (L + 1e-8),
                 )
 
-            early, late = range(0, E_PASSES // 2), range(E_PASSES // 2, E_PASSES)
+            return norms, normalise, flip, quantise, score, soften, add_up
+
+        def steps_among_passes(head, biased, square_sums):
+            norms, normalise, flip, quantise, score, soften, add_up = second_stage(
+                head,
+                biased,
+                square_sums,
+                lambda: psum.tile([P, BANK], F32, name="aux_bank", tag="aux"),
+            )
+            norms()
+            for c in range(E_PASSES):
+                for i in range(IMAGES):
+                    normalise(i, c)
+            half = E_PASSES // 2
+
+            def step_one():
+                for c in range(half):
+                    flip(c)
 
             def step_two():
-                quantise(early)
-                flip(late)
+                for c in range(half):
+                    quantise(c)
+                for c in range(half, E_PASSES):
+                    flip(c)
 
             def step_three():
-                quantise(late)
-                attend()
+                for c in range(half, E_PASSES):
+                    quantise(c)
+                for c in range(E_PASSES):
+                    score(c)
+                soften()
 
-            return [lambda: flip(early), step_two, step_three, add_up]
+            return [step_one, step_two, step_three, add_up]
+
+        def last_second_stage(head, biased, square_sums):
+            norms, normalise, flip, quantise, score, soften, add_up = second_stage(
+                head,
+                biased,
+                square_sums,
+                lambda: psum_sums.tile([P, BANK], F32, name="sums"),
+            )
+            norms()
+            for c in range(E_PASSES):
+                for i in range(IMAGES):
+                    normalise(i, c, on_scalar=(c == 0 and i == 1))
+            for c in range(E_PASSES):
+                flip(c)
+            for c in range(E_PASSES):
+                quantise(c)
+                score(c)
+            soften()
+            add_up()
 
         steps = []
         for number, (head, first_col, cols) in enumerate(rounds):
@@ -265,8 +357,8 @@ def tile_oaclipv3_w_e_kernel(tc, img1, img2, W_words, W_scales, b, out):
                             lhsT=img_codes[:, i, g, :].bitcast(FP8X4),
                             lhsT_scale=img_planes[:, i, g, :],
                             rhs=w_codes[:, g, BANK * c : BANK * (c + 1)].bitcast(FP8X4),
-                            rhs_scale=w_planes[
-                                4 * j : P, s, first_col + BANK * c : first_col + BANK * (c + 1)
+                            rhs_scale=w_planes[s][
+                                4 * j : P, first_col + BANK * c : first_col + BANK * (c + 1)
                             ],
                             start=(g == 0),
                             stop=(g == D_PASSES - 1),
@@ -296,10 +388,9 @@ def tile_oaclipv3_w_e_kernel(tc, img1, img2, W_words, W_scales, b, out):
                         func=ACT.Square,
                         accum_out=square_sums[:, i, block : block + 1],
                     )
-            if first_col + cols == E:
-                steps = second_stage_steps(head, biased, square_sums)
-        for step in steps:
-            step()
+            if first_col + cols == E and head < H - 1:
+                steps = steps_among_passes(head, biased, square_sums)
+        last_second_stage(H - 1, biased, square_sums)
 
         nc.sync.dma_start(
             out=out.flatten_outer_dims().rearrange("(o s) l -> o (s l)", o=1),

@@ -27,13 +27,18 @@ NORM_FLOOR = 1e-12
 D_PASSES = D // K_PASS
 E_PASSES = E // K_PASS
 BANK = 512
-ROUND_COLS = 1024
+ROUNDS = (
+    (0, 0, 2048, (0, 1, 2, 3, 4, 5, 6, 7)),
+    (1, 0, 1024, (0, 1, 2, 3)),
+    (1, 1024, 512, (4, 5)),
+    (1, 1536, 512, (0, 1)),
+)
+SIDE_BANKS = (6, 7)
 PLANES = 4
 PLANE_SETS = H * D_PASSES // PLANES
 IMAGE_CHUNKS = (slice(0, 1), slice(1, 2), slice(2, 4), slice(4, 6), slice(6, 8))
-W_BUFS = 3
-FIRST_STEP_AT = 7 * ROUND_COLS
-STEP_SPACING = 2 * ROUND_COLS
+FIRST_STEP_AT = 6 * 1024
+STEP_SPACING = 2 * 1024
 
 FLOPS = 2 * IMAGES * H * L * D * E + 2 * H * L * L * E
 
@@ -43,12 +48,14 @@ def tile_oaclipv3_w_e_kernel(tc, img1, img2, W_words, W_scales, b, out):
     images = (img1, img2)
     with ExitStack() as pools:
         const = pools.enter_context(tc.tile_pool(name="const", bufs=1))
-        weights = pools.enter_context(tc.tile_pool(name="weights", bufs=W_BUFS))
+        weights = pools.enter_context(tc.tile_pool(name="weights", bufs=1))
         work = pools.enter_context(tc.tile_pool(name="work", bufs=1))
         small = pools.enter_context(tc.tile_pool(name="small", bufs=2))
-        psum_sums = pools.enter_context(tc.psum_pool(name="psum_sums", bufs=6))
-        psum = pools.enter_context(tc.psum_pool(name="psum", bufs=2))
+        psum = pools.enter_context(tc.psum_pool(name="psum", bufs=1))
         pools.enter_context(tc.manual_schedule())
+
+        def bank_tile(number):
+            return psum.tile([P, BANK], F32, name="bank%d" % number)
 
         w_planes = [
             const.tile([P, E], U8, name="w_planes%d" % s, align_bytes=64) for s in range(PLANE_SETS)
@@ -91,8 +98,11 @@ def tile_oaclipv3_w_e_kernel(tc, img1, img2, W_words, W_scales, b, out):
                 .bitcast(I32),
             )
 
-        def load_round(head, first_col, cols, image_chunks={}, plane_sets={}):
-            w_codes = weights.tile([P, D_PASSES, cols], U32, name="w_codes", align_bytes=64)
+        def load_round(number, image_chunks={}, plane_sets={}):
+            head, first_col, cols, banks = ROUNDS[number]
+            w_codes = weights.tile(
+                [P, D_PASSES, cols], U32, name="w_codes%d" % number, align_bytes=64
+            )
             for g in range(D_PASSES):
                 if g in plane_sets:
                     load_plane_set(plane_sets[g])
@@ -101,12 +111,6 @@ def tile_oaclipv3_w_e_kernel(tc, img1, img2, W_words, W_scales, b, out):
                 load_pass(w_codes, head, g, first_col, cols)
             return w_codes
 
-        rounds = [
-            (head, first_col, ROUND_COLS) for head in range(H) for first_col in range(0, E, ROUND_COLS)
-        ]
-        head, first_col, cols = rounds.pop()
-        rounds += [(head, first_col, cols // 2), (head, first_col + cols // 2, cols // 2)]
-
         load_images(nc.scalar, IMAGE_CHUNKS[0])
         nc.scalar.dma_start(
             out=bias_rows[: H * E // BANK, :], in_=b.rearrange("h (c n) -> (h c) n", n=BANK)
@@ -114,17 +118,18 @@ def tile_oaclipv3_w_e_kernel(tc, img1, img2, W_words, W_scales, b, out):
         load_plane_set(0)
         loaded = [
             load_round(
-                *rounds[0],
+                0,
                 image_chunks={passes.start: passes for passes in IMAGE_CHUNKS[1:]},
-                plane_sets={PLANES: 1},
+                plane_sets={PLANES: 1, PLANES + 2: 2},
             ),
-            load_round(*rounds[1], plane_sets={2: 2, 6: 3}),
-            load_round(*rounds[2]),
+            load_round(1, plane_sets={0: 3}),
+            load_round(2),
+            load_round(3),
         ]
 
         bias_all = const.tile([P, H * E], BF16)
         for block in range(H * E // BANK):
-            spread = psum_sums.tile([P, BANK], F32, name="sums")
+            spread = bank_tile(block)
             nc.tensor.matmul(
                 spread[:],
                 lhsT=identity[:, block : block + 1].to_broadcast([P, P]),
@@ -155,84 +160,82 @@ def tile_oaclipv3_w_e_kernel(tc, img1, img2, W_words, W_scales, b, out):
         squares = const.tile([P, BANK], BF16)
         result = const.tile([P, 2, H, L], F32)
 
-        def second_stage(head, biased, square_sums, bank_tile):
+        def second_stage(head, biased, square_sums):
             inv_norm = small.tile([P, IMAGES], F32)
+            norm_sq = small.tile([P, IMAGES], F32)
             unit = [work.tile([P, E], BF16, name="unit%d" % i) for i in range(IMAGES)]
-            grouped_words = work.tile([P, E_PASSES, IMAGES, L, PACK // 2], F32, align_bytes=64)
-            unit_codes = work.tile([P, E_PASSES, IMAGES * L], U32, align_bytes=64)
-            unit_planes = work.tile([P, E_PASSES, IMAGES * L], U8, align_bytes=64)
+            grouped_words = work.tile([P, IMAGES, E_PASSES, L, PACK // 2], F32, align_bytes=64)
+            unit_codes = work.tile([P, IMAGES, E_PASSES, L], U32, align_bytes=64)
+            unit_planes = work.tile([P, IMAGES, E_PASSES, L], U8, align_bytes=64)
 
-            def norms():
-                rest = small.tile([P, IMAGES], F32)
+            def add_early_squares(i):
+                rest = small.tile([P, 1], F32, name="rest%d" % i)
                 nc.vector.tensor_reduce(
-                    out=rest[:], in_=square_sums[:, :, : E // BANK - 1], axis=AX.X, op=ALU.add
+                    out=rest[:], in_=square_sums[:, i, : E // BANK - 1], axis=AX.X, op=ALU.add
                 )
-                norm_sq = small.tile([P, IMAGES], F32)
-                for i in range(IMAGES):
-                    nc.vector.tensor_scalar(
-                        out=norm_sq[:, i : i + 1],
-                        in0=square_sums[:, i, E // BANK - 1 :],
-                        scalar1=rest[:, i : i + 1],
-                        scalar2=NORM_FLOOR * NORM_FLOOR,
-                        op0=ALU.add,
-                        op1=ALU.max,
-                    )
-                    nc.gpsimd.tensor_tensor(
-                        out=inv_norm[:, i : i + 1],
-                        in0=norm_sq[:, i : i + 1],
-                        in1=minus_half[:],
-                        op=ALU.pow,
-                    )
+                return rest
 
-            def normalise(i, c, on_scalar=False):
+            def invert_norm(i, rest):
+                nc.vector.tensor_scalar(
+                    out=norm_sq[:, i : i + 1],
+                    in0=square_sums[:, i, E // BANK - 1 :],
+                    scalar1=rest[:],
+                    scalar2=NORM_FLOOR * NORM_FLOOR,
+                    op0=ALU.add,
+                    op1=ALU.max,
+                )
+                nc.gpsimd.tensor_tensor(
+                    out=inv_norm[:, i : i + 1],
+                    in0=norm_sq[:, i : i + 1],
+                    in1=minus_half[:],
+                    op=ALU.pow,
+                )
+
+            def normalise(i, c):
                 cols = slice(K_PASS * c, K_PASS * (c + 1))
-                if on_scalar:
-                    nc.scalar.activation(
-                        out=unit[i][:, cols],
-                        in_=biased[i][:, cols],
-                        func=ACT.Copy,
-                        scale=inv_norm[:, i : i + 1],
-                    )
-                else:
-                    nc.vector.tensor_scalar_mul(
-                        out=unit[i][:, cols], in0=biased[i][:, cols], scalar1=inv_norm[:, i : i + 1]
-                    )
+                nc.vector.tensor_scalar_mul(
+                    out=unit[i][:, cols], in0=biased[i][:, cols], scalar1=inv_norm[:, i : i + 1]
+                )
 
-            def flip(c):
-                flipped = bank_tile()
-                flipped = flipped[:].rearrange("p (i u r) -> p i u r", i=IMAGES, u=PACK // 2)
-                for i in range(IMAGES):
-                    words = unit[i][:, K_PASS * c : K_PASS * (c + 1)].bitcast(F32)
+            def flip(i, passes, number):
+                count = passes.stop - passes.start
+                bank = bank_tile(number)
+                flipped = bank[:, : 2 * L * count].rearrange("p (c u r) -> p c u r", c=count, u=2)
+                words = unit[i][:].bitcast(F32)
+                for c in range(count):
                     for u in range(PACK // 2):
+                        first_word = K_PASS // 2 * (passes.start + c) + P * u
                         nc.tensor.transpose(
-                            flipped[:, i, u, :], words[:, P * u : P * (u + 1)], identity_words[:]
+                            flipped[:, c, u, :],
+                            words[:, first_word : first_word + P],
+                            identity_words[:],
                         )
                 nc.scalar.copy(
-                    out=grouped_words[:, c], in_=flipped.rearrange("p i u r -> p i r u")
+                    out=grouped_words[:, i, passes], in_=flipped.rearrange("p c u r -> p c r u")
                 )
 
-            def quantise(c):
+            def quantise(i, passes):
                 nc.vector.quantize_mx(
-                    out=unit_codes[:, c, :].bitcast(FP8X4),
-                    scales=unit_planes[:, c, :],
-                    in_=grouped_words[:, c].rearrange("p i r u -> p (i r u)").bitcast(BF16),
+                    out=unit_codes[:, i, passes].rearrange("p c r -> p (c r)").bitcast(FP8X4),
+                    scales=unit_planes[:, i, passes].rearrange("p c r -> p (c r)"),
+                    in_=grouped_words[:, i, passes]
+                    .rearrange("p c r u -> p (c r u)")
+                    .bitcast(BF16),
                 )
 
             scores = []
 
-            def score(c):
+            def score(c, numbers):
                 if c == 0:
-                    for which in range(2):
-                        scores.append(psum.tile([P, BANK], F32, name="scores", tag="aux"))
+                    for number in numbers:
+                        scores.append(bank_tile(number))
                 for which in range(2):
-                    rows = slice(L * (1 - which), L * (2 - which))
-                    free = slice(L * which, L * (which + 1))
                     nc.tensor.matmul_mx(
                         out=scores[which][:, :L],
-                        lhsT=unit_codes[:, c, rows].bitcast(FP8X4),
-                        lhsT_scale=unit_planes[:, c, rows],
-                        rhs=unit_codes[:, c, free].bitcast(FP8X4),
-                        rhs_scale=unit_planes[:, c, free],
+                        lhsT=unit_codes[:, 1 - which, c].bitcast(FP8X4),
+                        lhsT_scale=unit_planes[:, 1 - which, c],
+                        rhs=unit_codes[:, which, c].bitcast(FP8X4),
+                        rhs_scale=unit_planes[:, which, c],
                         start=(c == 0),
                         stop=(c == E_PASSES - 1),
                     )
@@ -268,8 +271,8 @@ def tile_oaclipv3_w_e_kernel(tc, img1, img2, W_words, W_scales, b, out):
                         out=inv_sum[:, which : which + 1], in_=row_sum[:, which : which + 1]
                     )
 
-            def add_up():
-                summed = bank_tile()
+            def add_up(number):
+                summed = bank_tile(number)
                 for which in range(2):
                     nc.tensor.matmul(
                         summed[:, L * which : L * (which + 1)],
@@ -284,113 +287,136 @@ def tile_oaclipv3_w_e_kernel(tc, img1, img2, W_words, W_scales, b, out):
                     scalar1=1.0 / (L + 1e-8),
                 )
 
-            return norms, normalise, flip, quantise, score, soften, add_up
-
-        def steps_among_passes(head, biased, square_sums):
-            norms, normalise, flip, quantise, score, soften, add_up = second_stage(
-                head,
-                biased,
-                square_sums,
-                lambda: psum.tile([P, BANK], F32, name="aux_bank", tag="aux"),
+            return (
+                add_early_squares, invert_norm, normalise, flip, quantise, score, soften, add_up
             )
-            norms()
-            for c in range(E_PASSES):
-                for i in range(IMAGES):
-                    normalise(i, c)
-            half = E_PASSES // 2
 
-            def step_one():
-                for c in range(half):
-                    flip(c)
+        halves = (slice(0, E_PASSES // 2), slice(E_PASSES // 2, E_PASSES))
+
+        def steps_among_passes(parts):
+            add_early_squares, invert_norm, normalise, flip, quantise, score, soften, add_up = parts
+
+            def flip_image(i):
+                for passes, number in zip(halves, SIDE_BANKS):
+                    flip(i, passes, number)
+
+            def quantise_image(i):
+                for passes in halves:
+                    quantise(i, passes)
 
             def step_two():
-                for c in range(half):
-                    quantise(c)
-                for c in range(half, E_PASSES):
-                    flip(c)
+                quantise_image(0)
+                flip_image(1)
 
             def step_three():
-                for c in range(half, E_PASSES):
-                    quantise(c)
+                quantise_image(1)
                 for c in range(E_PASSES):
-                    score(c)
+                    score(c, SIDE_BANKS)
                 soften()
 
-            return [step_one, step_two, step_three, add_up]
+            return [lambda: flip_image(0), step_two, step_three, lambda: add_up(SIDE_BANKS[0])]
 
-        def last_second_stage(head, biased, square_sums):
-            norms, normalise, flip, quantise, score, soften, add_up = second_stage(
-                head,
-                biased,
-                square_sums,
-                lambda: psum_sums.tile([P, BANK], F32, name="sums"),
+        def project(i, g, c):
+            s, j = divmod(D_PASSES * head + g, PLANES)
+            nc.tensor.matmul_mx(
+                out=sums[i][c][:],
+                lhsT=img_codes[:, i, g, :].bitcast(FP8X4),
+                lhsT_scale=img_planes[:, i, g, :],
+                rhs=w_codes[:, g, BANK * c : BANK * (c + 1)].bitcast(FP8X4),
+                rhs_scale=w_planes[s][
+                    4 * j : P, first_col + BANK * c : first_col + BANK * (c + 1)
+                ],
+                start=(g == 0),
+                stop=(g == D_PASSES - 1),
             )
-            norms()
-            for c in range(E_PASSES):
-                for i in range(IMAGES):
-                    normalise(i, c, on_scalar=(c == 0 and i == 1))
-            for c in range(E_PASSES):
-                flip(c)
-            for c in range(E_PASSES):
-                quantise(c)
-                score(c)
-            soften()
-            add_up()
+
+        def add_bias(i, c):
+            block = first_col // BANK + c
+            block_cols = slice(BANK * block, BANK * (block + 1))
+            nc.vector.tensor_tensor(
+                out=biased[i][:, block_cols],
+                in0=sums[i][c][:],
+                in1=bias_all[:, E * head + BANK * block : E * head + BANK * (block + 1)],
+                op=ALU.add,
+            )
+            nc.scalar.activation(
+                out=squares[:],
+                in_=biased[i][:, block_cols],
+                func=ACT.Square,
+                accum_out=square_sums[:, i, block : block + 1],
+            )
 
         steps = []
-        for number, (head, first_col, cols) in enumerate(rounds):
+        for number, (head, first_col, cols, banks) in enumerate(ROUNDS):
             w_codes = loaded[number]
-            banks = cols // BANK
+            blocks = cols // BANK
             if first_col == 0:
+                biased = [work.tile([P, E], F32, name="biased%d" % i) for i in range(IMAGES)]
+                square_sums = small.tile([P, IMAGES, E // BANK], F32)
                 written = 0
                 next_step_at = FIRST_STEP_AT
             sums = [
-                [psum_sums.tile([P, BANK], F32, name="sums") for c in range(banks)]
-                for i in range(IMAGES)
+                [bank_tile(banks[blocks * i + c]) for c in range(blocks)] for i in range(IMAGES)
             ]
-            for g in range(D_PASSES):
-                s, j = divmod(D_PASSES * head + g, PLANES)
+            last_round = number == len(ROUNDS) - 1
+            for g in range(D_PASSES // 2 if last_round else D_PASSES):
                 for i in range(IMAGES):
-                    for c in range(banks):
-                        nc.tensor.matmul_mx(
-                            out=sums[i][c][:],
-                            lhsT=img_codes[:, i, g, :].bitcast(FP8X4),
-                            lhsT_scale=img_planes[:, i, g, :],
-                            rhs=w_codes[:, g, BANK * c : BANK * (c + 1)].bitcast(FP8X4),
-                            rhs_scale=w_planes[s][
-                                4 * j : P, first_col + BANK * c : first_col + BANK * (c + 1)
-                            ],
-                            start=(g == 0),
-                            stop=(g == D_PASSES - 1),
-                        )
+                    for c in range(blocks):
+                        project(i, g, c)
                 written += cols
                 if steps and written >= next_step_at and g < D_PASSES - 1:
                     steps.pop(0)()
                     next_step_at += STEP_SPACING
-            if number + W_BUFS < len(rounds):
-                loaded.append(load_round(*rounds[number + W_BUFS]))
-            if first_col == 0:
-                biased = [work.tile([P, E], F32, name="biased%d" % i) for i in range(IMAGES)]
-                square_sums = small.tile([P, IMAGES, E // BANK], F32)
-            for i in range(IMAGES):
-                for c in range(banks):
-                    block = first_col // BANK + c
-                    block_cols = slice(BANK * block, BANK * (block + 1))
-                    nc.vector.tensor_tensor(
-                        out=biased[i][:, block_cols],
-                        in0=sums[i][c][:],
-                        in1=bias_all[:, E * head + BANK * block : E * head + BANK * (block + 1)],
-                        op=ALU.add,
-                    )
-                    nc.scalar.activation(
-                        out=squares[:],
-                        in_=biased[i][:, block_cols],
-                        func=ACT.Square,
-                        accum_out=square_sums[:, i, block : block + 1],
-                    )
-            if first_col + cols == E and head < H - 1:
-                steps = steps_among_passes(head, biased, square_sums)
-        last_second_stage(H - 1, biased, square_sums)
+            if head == 0:
+                parts = second_stage(head, biased, square_sums)
+                add_early_squares, invert_norm, normalise, flip, quantise, score, soften, add_up = (
+                    parts
+                )
+                for c in range(blocks):
+                    add_bias(0, c)
+                rest = add_early_squares(0)
+                add_bias(1, 0)
+                invert_norm(0, rest)
+                for c in range(1, blocks):
+                    add_bias(1, c)
+                for c in range(E_PASSES):
+                    normalise(0, c)
+                invert_norm(1, add_early_squares(1))
+                for c in range(E_PASSES):
+                    normalise(1, c)
+                steps = steps_among_passes(parts)
+            elif not last_round:
+                for i in range(IMAGES):
+                    for c in range(blocks):
+                        add_bias(i, c)
+
+        add_early_squares, invert_norm, normalise, flip, quantise, score, soften, add_up = (
+            second_stage(head, biased, square_sums)
+        )
+        for i in range(IMAGES):
+            for g in range(D_PASSES // 2, D_PASSES):
+                project(i, g, 0)
+        rest = [add_early_squares(i) for i in range(IMAGES)]
+        add_bias(0, 0)
+        invert_norm(0, rest[0])
+        add_bias(1, 0)
+        normalise(0, 0)
+        invert_norm(1, rest[1])
+        for c in range(1, E_PASSES):
+            normalise(0, c)
+        for c in range(E_PASSES):
+            normalise(1, c)
+        for passes, number in zip(halves, (2, 3)):
+            flip(0, passes, number)
+        for c, number in zip(range(E_PASSES), (4, 5, 6, 7)):
+            flip(1, slice(c, c + 1), number)
+        for passes in halves:
+            quantise(0, passes)
+        for c in range(E_PASSES):
+            quantise(1, slice(c, c + 1))
+            score(c, (0, 1))
+        soften()
+        add_up(2)
 
         nc.sync.dma_start(
             out=out.flatten_outer_dims().rearrange("(o s) l -> o (s l)", o=1),

@@ -31,9 +31,11 @@ ROUNDS = (
     (0, 0, 2048, (0, 1, 2, 3, 4, 5, 6, 7)),
     (1, 0, 1024, (0, 1, 2, 3)),
     (1, 1024, 512, (4, 5)),
-    (1, 1536, 512, (0, 1)),
+    (1, 1536, 512, ()),
 )
 SIDE_BANKS = (6, 7)
+LAST_PIECE_COLS = 256
+LAST_PIECES = 512 // LAST_PIECE_COLS
 PLANES = 4
 PLANE_SETS = H * D_PASSES // PLANES
 IMAGE_CHUNKS = (slice(0, 1), slice(1, 2), slice(2, 4), slice(4, 6), slice(6, 8))
@@ -120,9 +122,9 @@ def tile_oaclipv3_w_e_kernel(tc, img1, img2, W_words, W_scales, b, out):
             load_round(
                 0,
                 image_chunks={passes.start: passes for passes in IMAGE_CHUNKS[1:]},
-                plane_sets={PLANES: 1, PLANES + 2: 2},
+                plane_sets={PLANES: 1},
             ),
-            load_round(1, plane_sets={0: 3}),
+            load_round(1, plane_sets={0: 2, 2: 3}),
             load_round(2),
             load_round(3),
         ]
@@ -171,14 +173,14 @@ def tile_oaclipv3_w_e_kernel(tc, img1, img2, W_words, W_scales, b, out):
             def add_early_squares(i):
                 rest = small.tile([P, 1], F32, name="rest%d" % i)
                 nc.vector.tensor_reduce(
-                    out=rest[:], in_=square_sums[:, i, : E // BANK - 1], axis=AX.X, op=ALU.add
+                    out=rest[:], in_=square_sums[:, i, :-1], axis=AX.X, op=ALU.add
                 )
                 return rest
 
             def invert_norm(i, rest):
                 nc.vector.tensor_scalar(
                     out=norm_sq[:, i : i + 1],
-                    in0=square_sums[:, i, E // BANK - 1 :],
+                    in0=square_sums[:, i, square_sums.shape[2] - 1 :],
                     scalar1=rest[:],
                     scalar2=NORM_FLOOR * NORM_FLOOR,
                     op0=ALU.add,
@@ -316,107 +318,126 @@ def tile_oaclipv3_w_e_kernel(tc, img1, img2, W_words, W_scales, b, out):
 
             return [lambda: flip_image(0), step_two, step_three, lambda: add_up(SIDE_BANKS[0])]
 
-        def project(i, g, c):
+        def project(i, g, start_col, piece_cols, total):
             s, j = divmod(D_PASSES * head + g, PLANES)
             nc.tensor.matmul_mx(
-                out=sums[i][c][:],
+                out=total[:, :piece_cols],
                 lhsT=img_codes[:, i, g, :].bitcast(FP8X4),
                 lhsT_scale=img_planes[:, i, g, :],
-                rhs=w_codes[:, g, BANK * c : BANK * (c + 1)].bitcast(FP8X4),
+                rhs=w_codes[:, g, start_col : start_col + piece_cols].bitcast(FP8X4),
                 rhs_scale=w_planes[s][
-                    4 * j : P, first_col + BANK * c : first_col + BANK * (c + 1)
+                    4 * j : P, first_col + start_col : first_col + start_col + piece_cols
                 ],
                 start=(g == 0),
                 stop=(g == D_PASSES - 1),
             )
 
-        def add_bias(i, c):
-            block = first_col // BANK + c
-            block_cols = slice(BANK * block, BANK * (block + 1))
+        def add_bias(i, start_col, piece_cols, total, sum_column):
+            piece = slice(first_col + start_col, first_col + start_col + piece_cols)
             nc.vector.tensor_tensor(
-                out=biased[i][:, block_cols],
-                in0=sums[i][c][:],
-                in1=bias_all[:, E * head + BANK * block : E * head + BANK * (block + 1)],
+                out=biased[i][:, piece],
+                in0=total[:, :piece_cols],
+                in1=bias_all[:, E * head + piece.start : E * head + piece.stop],
                 op=ALU.add,
             )
             nc.scalar.activation(
-                out=squares[:],
-                in_=biased[i][:, block_cols],
+                out=squares[:, :piece_cols],
+                in_=biased[i][:, piece],
                 func=ACT.Square,
-                accum_out=square_sums[:, i, block : block + 1],
+                accum_out=square_sums[:, i, sum_column : sum_column + 1],
             )
 
         steps = []
-        for number, (head, first_col, cols, banks) in enumerate(ROUNDS):
+        for number, (head, first_col, cols, banks) in enumerate(ROUNDS[:-1]):
             w_codes = loaded[number]
             blocks = cols // BANK
             if first_col == 0:
                 biased = [work.tile([P, E], F32, name="biased%d" % i) for i in range(IMAGES)]
-                square_sums = small.tile([P, IMAGES, E // BANK], F32)
+                sum_columns = E // BANK + (LAST_PIECES - 1 if head == H - 1 else 0)
+                square_sums = small.tile([P, IMAGES, sum_columns], F32, name="squares%d" % head)
                 written = 0
                 next_step_at = FIRST_STEP_AT
             sums = [
                 [bank_tile(banks[blocks * i + c]) for c in range(blocks)] for i in range(IMAGES)
             ]
-            last_round = number == len(ROUNDS) - 1
-            for g in range(D_PASSES // 2 if last_round else D_PASSES):
+            for g in range(D_PASSES):
                 for i in range(IMAGES):
                     for c in range(blocks):
-                        project(i, g, c)
+                        project(i, g, BANK * c, BANK, sums[i][c])
                 written += cols
                 if steps and written >= next_step_at and g < D_PASSES - 1:
                     steps.pop(0)()
                     next_step_at += STEP_SPACING
+
+            def add_block_bias(i, c):
+                add_bias(i, BANK * c, BANK, sums[i][c], first_col // BANK + c)
+
             if head == 0:
                 parts = second_stage(head, biased, square_sums)
                 add_early_squares, invert_norm, normalise, flip, quantise, score, soften, add_up = (
                     parts
                 )
                 for c in range(blocks):
-                    add_bias(0, c)
+                    add_block_bias(0, c)
                 rest = add_early_squares(0)
-                add_bias(1, 0)
+                add_block_bias(1, 0)
                 invert_norm(0, rest)
                 for c in range(1, blocks):
-                    add_bias(1, c)
+                    add_block_bias(1, c)
                 for c in range(E_PASSES):
                     normalise(0, c)
                 invert_norm(1, add_early_squares(1))
                 for c in range(E_PASSES):
                     normalise(1, c)
                 steps = steps_among_passes(parts)
-            elif not last_round:
+            else:
                 for i in range(IMAGES):
                     for c in range(blocks):
-                        add_bias(i, c)
+                        add_block_bias(i, c)
 
+        head, first_col, cols, banks = ROUNDS[-1]
+        w_codes = loaded[-1]
         add_early_squares, invert_norm, normalise, flip, quantise, score, soften, add_up = (
             second_stage(head, biased, square_sums)
         )
+        last_sums = [[bank_tile(LAST_PIECES * i + c) for c in range(LAST_PIECES)] for i in range(IMAGES)]
         for i in range(IMAGES):
-            for g in range(D_PASSES // 2, D_PASSES):
-                project(i, g, 0)
-        rest = [add_early_squares(i) for i in range(IMAGES)]
-        add_bias(0, 0)
-        invert_norm(0, rest[0])
-        add_bias(1, 0)
-        normalise(0, 0)
-        invert_norm(1, rest[1])
-        for c in range(1, E_PASSES):
+            for c in range(LAST_PIECES):
+                for g in range(D_PASSES):
+                    project(i, g, LAST_PIECE_COLS * c, LAST_PIECE_COLS, last_sums[i][c])
+                    written += LAST_PIECE_COLS // IMAGES
+                    if steps and written >= next_step_at:
+                        steps.pop(0)()
+                        next_step_at += STEP_SPACING
+
+        def add_last_bias(i, c):
+            add_bias(
+                i, LAST_PIECE_COLS * c, LAST_PIECE_COLS, last_sums[i][c], first_col // BANK + c
+            )
+
+        for c in range(LAST_PIECES):
+            add_last_bias(0, c)
+        invert_norm(0, add_early_squares(0))
+        for c in range(LAST_PIECES):
+            add_last_bias(1, c)
+        rest = add_early_squares(1)
+        for c in range(E_PASSES // 2):
             normalise(0, c)
-        for c in range(E_PASSES):
-            normalise(1, c)
-        for passes, number in zip(halves, (2, 3)):
+        invert_norm(1, rest)
+        for c in range(E_PASSES // 2, E_PASSES):
+            normalise(0, c)
+        for passes, number in zip(halves, (4, 5)):
             flip(0, passes, number)
-        for c, number in zip(range(E_PASSES), (4, 5, 6, 7)):
+        quantise(0, halves[0])
+        for c, number in zip(range(E_PASSES), (6, 7, 0, 1)):
+            normalise(1, c)
             flip(1, slice(c, c + 1), number)
-        for passes in halves:
-            quantise(0, passes)
+        quantise(0, halves[1])
         for c in range(E_PASSES):
             quantise(1, slice(c, c + 1))
-            score(c, (0, 1))
+            score(c, (2, 3))
         soften()
-        add_up(2)
+        add_up(4)
 
         nc.sync.dma_start(
             out=out.flatten_outer_dims().rearrange("(o s) l -> o (s l)", o=1),

@@ -74,12 +74,16 @@ def tile_oaclipv3_w_e_kernel(tc, img1, img2, W_words, W_scales, b, out):
         identity_words = const.tile([P, P], F32)
         make_identity(nc, identity_words[:])
 
-        def load_plane_set(s):
+        def load_plane_set(s, first_col, cols):
             for quadrant in range(4):
                 nc.sync.dma_start(
-                    out=w_planes[s][32 * quadrant : 32 * quadrant + 4 * PLANES, :].bitcast(I32),
+                    out=w_planes[s][
+                        32 * quadrant : 32 * quadrant + 4 * PLANES, first_col : first_col + cols
+                    ].bitcast(I32),
                     in_=W_scales[
-                        PLANES * s : PLANES * (s + 1), 4 * quadrant : 4 * quadrant + 4, :
+                        PLANES * s : PLANES * (s + 1),
+                        4 * quadrant : 4 * quadrant + 4,
+                        first_col : first_col + cols,
                     ].bitcast(I32),
                 )
 
@@ -107,7 +111,7 @@ def tile_oaclipv3_w_e_kernel(tc, img1, img2, W_words, W_scales, b, out):
             )
             for g in range(D_PASSES):
                 if g in plane_sets:
-                    load_plane_set(plane_sets[g])
+                    load_plane_set(*plane_sets[g])
                 if g in image_chunks:
                     load_images(nc.sync, image_chunks[g])
                 load_pass(w_codes, head, g, first_col, cols)
@@ -117,15 +121,15 @@ def tile_oaclipv3_w_e_kernel(tc, img1, img2, W_words, W_scales, b, out):
         nc.scalar.dma_start(
             out=bias_rows[: H * E // BANK, :], in_=b.rearrange("h (c n) -> (h c) n", n=BANK)
         )
-        load_plane_set(0)
+        load_plane_set(0, 0, E)
         loaded = [
             load_round(
                 0,
                 image_chunks={passes.start: passes for passes in IMAGE_CHUNKS[1:]},
-                plane_sets={PLANES: 1},
+                plane_sets={PLANES: (1, 0, E)},
             ),
-            load_round(1, plane_sets={0: 2, 2: 3}),
-            load_round(2),
+            load_round(1, plane_sets={0: (2, 0, E // 2), 2: (3, 0, E // 2)}),
+            load_round(2, plane_sets={0: (2, E // 2, E // 2), 2: (3, E // 2, E // 2)}),
             load_round(3),
         ]
 
@@ -428,11 +432,11 @@ def tile_oaclipv3_w_e_kernel(tc, img1, img2, W_words, W_scales, b, out):
             normalise(0, c)
         for passes, number in zip(halves, (4, 5)):
             flip(0, passes, number)
-        quantise(0, halves[0])
-        for c, number in zip(range(E_PASSES), (6, 7, 0, 1)):
-            normalise(1, c)
-            flip(1, slice(c, c + 1), number)
-        quantise(0, halves[1])
+        for half, passes in enumerate(halves):
+            for c in range(passes.start, passes.stop):
+                normalise(1, c)
+                flip(1, slice(c, c + 1), (6, 7, 0, 1)[c])
+            quantise(0, passes)
         for c in range(E_PASSES):
             quantise(1, slice(c, c + 1))
             score(c, (2, 3))

@@ -405,14 +405,17 @@ def tile_oaclipv3_w_e_kernel(tc, img1, img2, W_words, W_scales, b, out):
             second_stage(head, biased, square_sums)
         )
         last_sums = [[bank_tile(LAST_PIECES * i + c) for c in range(LAST_PIECES)] for i in range(IMAGES)]
-        for i in range(IMAGES):
-            for c in range(LAST_PIECES):
-                for g in range(D_PASSES):
-                    project(i, g, LAST_PIECE_COLS * c, LAST_PIECE_COLS, last_sums[i][c])
-                    written += LAST_PIECE_COLS // IMAGES
-                    if steps and written >= next_step_at:
-                        steps.pop(0)()
-                        next_step_at += STEP_SPACING
+        for passes in (range(D_PASSES // 2), range(D_PASSES // 2, D_PASSES)):
+            if passes.start == 0:
+                order = [(i, g, c) for g in passes for i in range(IMAGES) for c in range(LAST_PIECES)]
+            else:
+                order = [(i, g, c) for i in range(IMAGES) for c in range(LAST_PIECES) for g in passes]
+            for i, g, c in order:
+                project(i, g, LAST_PIECE_COLS * c, LAST_PIECE_COLS, last_sums[i][c])
+                written += LAST_PIECE_COLS // IMAGES
+                if steps and written >= next_step_at:
+                    steps.pop(0)()
+                    next_step_at += STEP_SPACING
 
         def add_last_bias(i, c):
             add_bias(

@@ -231,47 +231,47 @@ def tile_oaclipv3_w_e_kernel(tc, img1, img2, W_words, W_scales, b, out):
 
             scores = []
 
-            def score(c, numbers):
-                if c == 0:
-                    for number in numbers:
-                        scores.append(bank_tile(number))
-                for which in range(2):
-                    nc.tensor.matmul_mx(
-                        out=scores[which][:, :L],
-                        lhsT=unit_codes[:, 1 - which, c].bitcast(FP8X4),
-                        lhsT_scale=unit_planes[:, 1 - which, c],
-                        rhs=unit_codes[:, which, c].bitcast(FP8X4),
-                        rhs_scale=unit_planes[:, which, c],
-                        start=(c == 0),
-                        stop=(c == E_PASSES - 1),
-                    )
+            def score(which, c):
+                nc.tensor.matmul_mx(
+                    out=scores[which],
+                    lhsT=unit_codes[:, 1 - which, c].bitcast(FP8X4),
+                    lhsT_scale=unit_planes[:, 1 - which, c],
+                    rhs=unit_codes[:, which, c].bitcast(FP8X4),
+                    rhs_scale=unit_planes[:, which, c],
+                    start=(c == 0),
+                    stop=(c == E_PASSES - 1),
+                )
 
             weight = small.tile([P, 2, L], F32)
+            shift = small.tile([P, 2], F32)
+            row_sum = small.tile([P, 2], F32)
             inv_sum = small.tile([P, 2], F32)
 
-            def soften():
-                shift = small.tile([P, 2], F32)
-                row_sum = small.tile([P, 2], F32)
+            def find_shifts():
                 for which in range(2):
                     negated = small.tile([P, L], F32)
                     nc.vector.tensor_scalar(
                         out=negated[:],
-                        in0=scores[which][:, :L],
+                        in0=scores[which],
                         scalar1=-LAMBDA_ATTN,
                         scalar2=None,
                         op0=ALU.mult,
                         op1=ALU.min,
                         accum_out=shift[:, which : which + 1],
                     )
+
+            def exponentiate():
                 for which in range(2):
                     nc.scalar.activation(
                         out=weight[:, which, :],
-                        in_=scores[which][:, :L],
+                        in_=scores[which],
                         func=ACT.Exp,
                         bias=shift[:, which : which + 1],
                         scale=LAMBDA_ATTN,
                         accum_out=row_sum[:, which : which + 1],
                     )
+
+            def invert_sums():
                 for which in range(2):
                     nc.vector.reciprocal(
                         out=inv_sum[:, which : which + 1], in_=row_sum[:, which : which + 1]
@@ -287,40 +287,38 @@ def tile_oaclipv3_w_e_kernel(tc, img1, img2, W_words, W_scales, b, out):
                         start=True,
                         stop=True,
                     )
-                nc.vector.tensor_scalar_mul(
-                    out=result[:, :, head, :],
-                    in0=summed[:, : 2 * L].rearrange("p (w l) -> p w l", w=2),
-                    scalar1=1.0 / (L + 1e-8),
-                )
+                return summed[:, : 2 * L].rearrange("p (w l) -> p w l", w=2)
 
-            return (
-                add_early_squares, invert_norm, normalise, flip, quantise, score, soften, add_up
-            )
+            return {
+                "add_early_squares": add_early_squares,
+                "invert_norm": invert_norm,
+                "normalise": normalise,
+                "flip": flip,
+                "quantise": quantise,
+                "scores": scores,
+                "score": score,
+                "find_shifts": find_shifts,
+                "exponentiate": exponentiate,
+                "invert_sums": invert_sums,
+                "add_up": add_up,
+            }
 
         halves = (slice(0, E_PASSES // 2), slice(E_PASSES // 2, E_PASSES))
 
-        def steps_among_passes(parts):
-            add_early_squares, invert_norm, normalise, flip, quantise, score, soften, add_up = parts
-
+        def steps_among_passes(stage):
             def flip_image(i):
                 for passes, number in zip(halves, SIDE_BANKS):
-                    flip(i, passes, number)
+                    stage["flip"](i, passes, number)
 
             def quantise_image(i):
                 for passes in halves:
-                    quantise(i, passes)
+                    stage["quantise"](i, passes)
 
             def step_two():
                 quantise_image(0)
                 flip_image(1)
 
-            def step_three():
-                quantise_image(1)
-                for c in range(E_PASSES):
-                    score(c, SIDE_BANKS)
-                soften()
-
-            return [lambda: flip_image(0), step_two, step_three, lambda: add_up(SIDE_BANKS[0])]
+            return [lambda: flip_image(0), step_two, lambda: quantise_image(1)]
 
         def project(i, g, start_col, piece_cols, total):
             s, j = divmod(D_PASSES * head + g, PLANES)
@@ -377,23 +375,20 @@ def tile_oaclipv3_w_e_kernel(tc, img1, img2, W_words, W_scales, b, out):
                 add_bias(i, BANK * c, BANK, sums[i][c], first_col // BANK + c)
 
             if head == 0:
-                parts = second_stage(head, biased, square_sums)
-                add_early_squares, invert_norm, normalise, flip, quantise, score, soften, add_up = (
-                    parts
-                )
+                first_stage = stage = second_stage(head, biased, square_sums)
                 for c in range(blocks):
                     add_block_bias(0, c)
-                rest = add_early_squares(0)
+                rest = stage["add_early_squares"](0)
                 add_block_bias(1, 0)
-                invert_norm(0, rest)
+                stage["invert_norm"](0, rest)
                 for c in range(1, blocks):
                     add_block_bias(1, c)
                 for c in range(E_PASSES):
-                    normalise(0, c)
-                invert_norm(1, add_early_squares(1))
+                    stage["normalise"](0, c)
+                stage["invert_norm"](1, stage["add_early_squares"](1))
                 for c in range(E_PASSES):
-                    normalise(1, c)
-                steps = steps_among_passes(parts)
+                    stage["normalise"](1, c)
+                steps = steps_among_passes(stage)
             else:
                 for i in range(IMAGES):
                     for c in range(blocks):
@@ -401,9 +396,7 @@ def tile_oaclipv3_w_e_kernel(tc, img1, img2, W_words, W_scales, b, out):
 
         head, first_col, cols, banks = ROUNDS[-1]
         w_codes = loaded[-1]
-        add_early_squares, invert_norm, normalise, flip, quantise, score, soften, add_up = (
-            second_stage(head, biased, square_sums)
-        )
+        stage = second_stage(head, biased, square_sums)
         last_sums = [[bank_tile(LAST_PIECES * i + c) for c in range(LAST_PIECES)] for i in range(IMAGES)]
         for passes in (range(D_PASSES // 2), range(D_PASSES // 2, D_PASSES)):
             if passes.start == 0:
@@ -412,10 +405,12 @@ def tile_oaclipv3_w_e_kernel(tc, img1, img2, W_words, W_scales, b, out):
                 order = [(i, g, c) for i in range(IMAGES) for c in range(LAST_PIECES) for g in passes]
             for i, g, c in order:
                 project(i, g, LAST_PIECE_COLS * c, LAST_PIECE_COLS, last_sums[i][c])
-                written += LAST_PIECE_COLS // IMAGES
-                if steps and written >= next_step_at:
-                    steps.pop(0)()
-                    next_step_at += STEP_SPACING
+
+        first_scores = bank_tile(6)
+        for which in range(2):
+            first_stage["scores"].append(first_scores[:, L * which : L * (which + 1)])
+            for c in range(E_PASSES):
+                first_stage["score"](which, c)
 
         def add_last_bias(i, c):
             add_bias(
@@ -424,27 +419,43 @@ def tile_oaclipv3_w_e_kernel(tc, img1, img2, W_words, W_scales, b, out):
 
         for c in range(LAST_PIECES):
             add_last_bias(0, c)
-        invert_norm(0, add_early_squares(0))
+        stage["invert_norm"](0, stage["add_early_squares"](0))
         for c in range(LAST_PIECES):
             add_last_bias(1, c)
-        rest = add_early_squares(1)
+        rest = stage["add_early_squares"](1)
         for c in range(E_PASSES // 2):
-            normalise(0, c)
-        invert_norm(1, rest)
+            stage["normalise"](0, c)
+        stage["invert_norm"](1, rest)
         for c in range(E_PASSES // 2, E_PASSES):
-            normalise(0, c)
+            stage["normalise"](0, c)
+        first_stage["find_shifts"]()
         for passes, number in zip(halves, (4, 5)):
-            flip(0, passes, number)
-        for half, passes in enumerate(halves):
+            stage["flip"](0, passes, number)
+        for passes in halves:
             for c in range(passes.start, passes.stop):
-                normalise(1, c)
-                flip(1, slice(c, c + 1), (6, 7, 0, 1)[c])
-            quantise(0, passes)
+                stage["normalise"](1, c)
+                stage["flip"](1, slice(c, c + 1), (7, 0, 1, 2)[c])
+            stage["quantise"](0, passes)
+        first_stage["exponentiate"]()
+        for number in (3, 4):
+            scores = bank_tile(number)
+            stage["scores"].append(scores[:, :L])
         for c in range(E_PASSES):
-            quantise(1, slice(c, c + 1))
-            score(c, (2, 3))
-        soften()
-        add_up(4)
+            stage["quantise"](1, slice(c, c + 1))
+            for which in range(2):
+                stage["score"](which, c)
+        stage["find_shifts"]()
+        first_stage["invert_sums"]()
+        stage["exponentiate"]()
+        stage["invert_sums"]()
+
+        first_total, total = first_stage["add_up"](5), stage["add_up"](6)
+        nc.scalar.activation(
+            out=result[:, :, 0, :], in_=first_total, func=ACT.Copy, scale=1.0 / (L + 1e-8)
+        )
+        nc.vector.tensor_scalar_mul(
+            out=result[:, :, 1, :], in0=total, scalar1=1.0 / (L + 1e-8)
+        )
 
         nc.sync.dma_start(
             out=out.flatten_outer_dims().rearrange("(o s) l -> o (s l)", o=1),

@@ -38,9 +38,11 @@ LAST_PIECE_COLS = 256
 LAST_PIECES = 512 // LAST_PIECE_COLS
 PLANES = 4
 PLANE_SETS = H * D_PASSES // PLANES
-IMAGE_CHUNKS = (slice(0, 1), slice(1, 2), slice(2, 4), slice(4, 6), slice(6, 8))
+IMAGE_CHUNKS = tuple(slice(g, g + 1) for g in range(8))
 FIRST_STEP_AT = 6 * 1024
 STEP_SPACING = 2 * 1024
+
+OPERAND_ALIGN = 256
 
 FLOPS = 2 * IMAGES * H * L * D * E + 2 * H * L * L * E
 
@@ -60,7 +62,7 @@ def tile_oaclipv3_w_e_kernel(tc, img1, img2, W_words, W_scales, b, out):
             return psum.tile([P, BANK], F32, name="bank%d" % number)
 
         w_planes = [
-            const.tile([P, E], U8, name="w_planes%d" % s, align_bytes=64) for s in range(PLANE_SETS)
+            const.tile([P, E], U8, name="w_planes%d" % s, align_bytes=OPERAND_ALIGN) for s in range(PLANE_SETS)
         ]
         nc.vector.memset(w_planes[0][:].bitcast(I32), 0)
         bias_rows = const.tile([P, BANK], BF16)
@@ -107,7 +109,7 @@ def tile_oaclipv3_w_e_kernel(tc, img1, img2, W_words, W_scales, b, out):
         def load_round(number, image_chunks={}, plane_sets={}):
             head, first_col, cols, banks = ROUNDS[number]
             w_codes = weights.tile(
-                [P, D_PASSES, cols], U32, name="w_codes%d" % number, align_bytes=64
+                [P, D_PASSES, cols], U32, name="w_codes%d" % number, align_bytes=OPERAND_ALIGN
             )
             for g in range(D_PASSES):
                 if g in plane_sets:
@@ -145,10 +147,10 @@ def tile_oaclipv3_w_e_kernel(tc, img1, img2, W_words, W_scales, b, out):
             )
             nc.scalar.copy(out=bias_all[:, BANK * block : BANK * (block + 1)], in_=spread[:])
 
-        img_codes = const.tile([P, IMAGES, D_PASSES, L], U32, align_bytes=64)
-        img_planes = const.tile([P, IMAGES, D_PASSES, L], U8, align_bytes=64)
+        img_codes = const.tile([P, IMAGES, D_PASSES, L], U32, align_bytes=OPERAND_ALIGN)
+        img_planes = const.tile([P, IMAGES, D_PASSES, L], U8, align_bytes=OPERAND_ALIGN)
         grouped = [
-            const.tile([P, D_PASSES, L, PACK], BF16, name="grouped%d" % i, align_bytes=64)
+            const.tile([P, D_PASSES, L, PACK], BF16, name="grouped%d" % i, align_bytes=OPERAND_ALIGN)
             for i in range(IMAGES)
         ]
         for passes in IMAGE_CHUNKS:
@@ -170,9 +172,9 @@ def tile_oaclipv3_w_e_kernel(tc, img1, img2, W_words, W_scales, b, out):
             inv_norm = small.tile([P, IMAGES], F32)
             norm_sq = small.tile([P, IMAGES], F32)
             unit = [work.tile([P, E], BF16, name="unit%d" % i) for i in range(IMAGES)]
-            grouped_words = work.tile([P, IMAGES, E_PASSES, L, PACK // 2], F32, align_bytes=64)
-            unit_codes = work.tile([P, IMAGES, E_PASSES, L], U32, align_bytes=64)
-            unit_planes = work.tile([P, IMAGES, E_PASSES, L], U8, align_bytes=64)
+            grouped_words = work.tile([P, IMAGES, E_PASSES, L, PACK // 2], F32, align_bytes=OPERAND_ALIGN)
+            unit_codes = work.tile([P, IMAGES, E_PASSES, L], U32, align_bytes=OPERAND_ALIGN)
+            unit_planes = work.tile([P, IMAGES, E_PASSES, L], U8, align_bytes=OPERAND_ALIGN)
 
             def add_early_squares(i):
                 rest = small.tile([P, 1], F32, name="rest%d" % i)
@@ -197,11 +199,19 @@ def tile_oaclipv3_w_e_kernel(tc, img1, img2, W_words, W_scales, b, out):
                     op=ALU.pow,
                 )
 
-            def normalise(i, c):
+            def normalise(i, c, on_scalar=False):
                 cols = slice(K_PASS * c, K_PASS * (c + 1))
-                nc.vector.tensor_scalar_mul(
-                    out=unit[i][:, cols], in0=biased[i][:, cols], scalar1=inv_norm[:, i : i + 1]
-                )
+                if on_scalar:
+                    nc.scalar.activation(
+                        out=unit[i][:, cols],
+                        in_=biased[i][:, cols],
+                        func=ACT.Copy,
+                        scale=inv_norm[:, i : i + 1],
+                    )
+                else:
+                    nc.vector.tensor_scalar_mul(
+                        out=unit[i][:, cols], in0=biased[i][:, cols], scalar1=inv_norm[:, i : i + 1]
+                    )
 
             def flip(i, passes, number):
                 count = passes.stop - passes.start
@@ -277,17 +287,16 @@ def tile_oaclipv3_w_e_kernel(tc, img1, img2, W_words, W_scales, b, out):
                         out=inv_sum[:, which : which + 1], in_=row_sum[:, which : which + 1]
                     )
 
-            def add_up(number):
+            def add_up(which, number):
                 summed = bank_tile(number)
-                for which in range(2):
-                    nc.tensor.matmul(
-                        summed[:, L * which : L * (which + 1)],
-                        lhsT=inv_sum[:, which : which + 1].to_broadcast([P, P]),
-                        rhs=weight[:, which, :],
-                        start=True,
-                        stop=True,
-                    )
-                return summed[:, : 2 * L].rearrange("p (w l) -> p w l", w=2)
+                nc.tensor.matmul(
+                    summed[:, :L],
+                    lhsT=inv_sum[:, which : which + 1].to_broadcast([P, P]),
+                    rhs=weight[:, which, :],
+                    start=True,
+                    stop=True,
+                )
+                return summed[:, :L]
 
             return {
                 "add_early_squares": add_early_squares,
@@ -426,36 +435,39 @@ def tile_oaclipv3_w_e_kernel(tc, img1, img2, W_words, W_scales, b, out):
         for c in range(E_PASSES // 2):
             stage["normalise"](0, c)
         stage["invert_norm"](1, rest)
-        for c in range(E_PASSES // 2, E_PASSES):
-            stage["normalise"](0, c)
         first_stage["find_shifts"]()
-        for passes, number in zip(halves, (4, 5)):
-            stage["flip"](0, passes, number)
+        stage["normalise"](0, 2)
+        stage["normalise"](0, 3, on_scalar=True)
+        for c in range(E_PASSES):
+            stage["flip"](0, slice(c, c + 1), (4, 5, 7, 0)[c])
         for passes in halves:
             for c in range(passes.start, passes.stop):
                 stage["normalise"](1, c)
-                stage["flip"](1, slice(c, c + 1), (7, 0, 1, 2)[c])
+                stage["flip"](1, slice(c, c + 1), (1, 2, 4, 5)[c])
             stage["quantise"](0, passes)
         first_stage["exponentiate"]()
-        for number in (3, 4):
+        for number in (3, 7):
             scores = bank_tile(number)
             stage["scores"].append(scores[:, :L])
         for c in range(E_PASSES):
             stage["quantise"](1, slice(c, c + 1))
             for which in range(2):
                 stage["score"](which, c)
-        stage["find_shifts"]()
         first_stage["invert_sums"]()
+        stage["find_shifts"]()
         stage["exponentiate"]()
         stage["invert_sums"]()
 
-        first_total, total = first_stage["add_up"](5), stage["add_up"](6)
-        nc.scalar.activation(
-            out=result[:, :, 0, :], in_=first_total, func=ACT.Copy, scale=1.0 / (L + 1e-8)
-        )
-        nc.vector.tensor_scalar_mul(
-            out=result[:, :, 1, :], in0=total, scalar1=1.0 / (L + 1e-8)
-        )
+        for which, number in zip(range(2), (0, 1)):
+            total = first_stage["add_up"](which, number)
+            nc.scalar.activation(
+                out=result[:, which, 0, :], in_=total, func=ACT.Copy, scale=1.0 / (L + 1e-8)
+            )
+        for which, number in zip(range(2), (2, 4)):
+            total = stage["add_up"](which, number)
+            nc.vector.tensor_scalar_mul(
+                out=result[:, which, 1, :], in0=total, scalar1=1.0 / (L + 1e-8)
+            )
 
         nc.sync.dma_start(
             out=out.flatten_outer_dims().rearrange("(o s) l -> o (s l)", o=1),

from contextlib import ExitStack

import concourse.mybir as mybir
from concourse.masks import make_identity

F32 = mybir.dt.float32
BF16 = mybir.dt.bfloat16
I32 = mybir.dt.int32
U32 = mybir.dt.uint32
U8 = mybir.dt.uint8
FP8X4 = mybir.dt.float8_e4m3fn_x4
ALU = mybir.AluOpType
ACT = mybir.ActivationFunctionType
AX = mybir.AxisListType

P = 128
PACK = 4
K_PASS = P * PACK
L = 128
D = 4096
E = 2048
H = 2
IMAGES = 2
LAMBDA_ATTN = 10.0
NORM_FLOOR = 1e-12

D_PASSES = D // K_PASS
E_PASSES = E // K_PASS
BANK = 512
ROUNDS = (
    (0, 0, 2048, (0, 1, 2, 3, 4, 5, 6, 7)),
    (1, 0, 1024, (0, 1, 2, 3)),
    (1, 1024, 512, (4, 5)),
    (1, 1536, 512, ()),
)
SIDE_BANKS = (6, 7)
LAST_PIECE_COLS = 256
LAST_PIECES = 512 // LAST_PIECE_COLS
PLANES = 4
PLANE_SETS = H * D_PASSES // PLANES
IMAGE_CHUNKS = tuple(slice(g, g + 1) for g in range(8))
FIRST_STEP_AT = 6 * 1024
STEP_SPACING = 2 * 1024

OPERAND_ALIGN = 256

FLOPS = 2 * IMAGES * H * L * D * E + 2 * H * L * L * E


def tile_oaclipv3_w_e_kernel(tc, img1, img2, W_words, W_scales, b, out):
    nc = tc.nc
    images = (img1, img2)
    with ExitStack() as pools:
        const = pools.enter_context(tc.tile_pool(name="const", bufs=1))
        weights = pools.enter_context(tc.tile_pool(name="weights", bufs=1))
        work = pools.enter_context(tc.tile_pool(name="work", bufs=1))
        small = pools.enter_context(tc.tile_pool(name="small", bufs=2))
        psum = pools.enter_context(tc.psum_pool(name="psum", bufs=1))
        pools.enter_context(tc.manual_schedule())

        def bank_tile(number):
            return psum.tile([P, BANK], F32, name="bank%d" % number)

        w_planes = [
            const.tile([P, E], U8, name="w_planes%d" % s, align_bytes=OPERAND_ALIGN) for s in range(PLANE_SETS)
        ]
        nc.vector.memset(w_planes[0][:].bitcast(I32), 0)
        bias_rows = const.tile([P, BANK], BF16)
        nc.vector.memset(bias_rows[:].bitcast(I32), 0)
        minus_half = const.tile([P, 1], F32)
        nc.vector.memset(minus_half[:], -0.5)
        for s in range(1, PLANE_SETS):
            nc.vector.memset(w_planes[s][:].bitcast(I32), 0)
        identity = const.tile([P, P], BF16)
        make_identity(nc, identity[:])
        identity_words = const.tile([P, P], F32)
        make_identity(nc, identity_words[:])

        def load_plane_set(s, first_col, cols):
            for quadrant in range(4):
                nc.sync.dma_start(
                    out=w_planes[s][
                        32 * quadrant : 32 * quadrant + 4 * PLANES, first_col : first_col + cols
                    ].bitcast(I32),
                    in_=W_scales[
                        PLANES * s : PLANES * (s + 1),
                        4 * quadrant : 4 * quadrant + 4,
                        first_col : first_col + cols,
                    ].bitcast(I32),
                )

        raw = [const.tile([P, D_PASSES, PACK, L], BF16, name="raw%d" % i) for i in range(IMAGES)]

        def load_images(queue, passes):
            for i in range(IMAGES):
                queue.dma_start(
                    out=raw[i][:, passes],
                    in_=images[i][0].rearrange("(g p t) r -> p g t r", p=P, t=PACK)[:, passes],
                )

        def load_pass(w_codes, head, g, first_col, cols):
            nc.sync.dma_start(
                out=w_codes[:, g, :].bitcast(I32),
                in_=W_words[D_PASSES * head + g]
                .rearrange("p n t -> p (n t)")[:, PACK * first_col : PACK * (first_col + cols)]
                .bitcast(I32),
            )

        def load_round(number, image_chunks={}, plane_sets={}):
            head, first_col, cols, banks = ROUNDS[number]
            w_codes = weights.tile(
                [P, D_PASSES, cols], U32, name="w_codes%d" % number, align_bytes=OPERAND_ALIGN
            )
            for g in range(D_PASSES):
                if g in plane_sets:
                    load_plane_set(*plane_sets[g])
                if g in image_chunks:
                    load_images(nc.sync, image_chunks[g])
                load_pass(w_codes, head, g, first_col, cols)
            return w_codes

        load_images(nc.scalar, IMAGE_CHUNKS[0])
        nc.scalar.dma_start(
            out=bias_rows[: H * E // BANK, :], in_=b.rearrange("h (c n) -> (h c) n", n=BANK)
        )
        load_plane_set(0, 0, E)
        loaded = [
            load_round(
                0,
                image_chunks={passes.start: passes for passes in IMAGE_CHUNKS[1:]},
                plane_sets={PLANES: (1, 0, E)},
            ),
            load_round(1, plane_sets={0: (2, 0, E // 2), 2: (3, 0, E // 2)}),
            load_round(2, plane_sets={0: (2, E // 2, E // 2), 2: (3, E // 2, E // 2)}),
            load_round(3),
        ]

        bias_all = const.tile([P, H * E], BF16)
        for block in range(H * E // BANK):
            spread = bank_tile(block)
            nc.tensor.matmul(
                spread[:],
                lhsT=identity[:, block : block + 1].to_broadcast([P, P]),
                rhs=bias_rows[:],
                start=True,
                stop=True,
            )
            nc.scalar.copy(out=bias_all[:, BANK * block : BANK * (block + 1)], in_=spread[:])

        img_codes = const.tile([P, IMAGES, D_PASSES, L], U32, align_bytes=OPERAND_ALIGN)
        img_planes = const.tile([P, IMAGES, D_PASSES, L], U8, align_bytes=OPERAND_ALIGN)
        grouped = [
            const.tile([P, D_PASSES, L, PACK], BF16, name="grouped%d" % i, align_bytes=OPERAND_ALIGN)
            for i in range(IMAGES)
        ]
        for passes in IMAGE_CHUNKS:
            for i in range(IMAGES):
                nc.vector.tensor_copy(
                    out=grouped[i][:, passes], in_=raw[i][:, passes].rearrange("p g t r -> p g r t")
                )
            for i in range(IMAGES):
                nc.vector.quantize_mx(
                    out=img_codes[:, i, passes].rearrange("p g r -> p (g r)").bitcast(FP8X4),
                    scales=img_planes[:, i, passes].rearrange("p g r -> p (g r)"),
                    in_=grouped[i][:, passes].rearrange("p g r t -> p (g r t)"),
                )

        squares = const.tile([P, BANK], BF16)
        result = const.tile([P, 2, H, L], F32)

        def second_stage(head, biased, square_sums):
            inv_norm = small.tile([P, IMAGES], F32)
            norm_sq = small.tile([P, IMAGES], F32)
            unit = [work.tile([P, E], BF16, name="unit%d" % i) for i in range(IMAGES)]
            grouped_words = work.tile([P, IMAGES, E_PASSES, L, PACK // 2], F32, align_bytes=OPERAND_ALIGN)
            unit_codes = work.tile([P, IMAGES, E_PASSES, L], U32, align_bytes=OPERAND_ALIGN)
            unit_planes = work.tile([P, IMAGES, E_PASSES, L], U8, align_bytes=OPERAND_ALIGN)

            def add_early_squares(i):
                rest = small.tile([P, 1], F32, name="rest%d" % i)
                nc.vector.tensor_reduce(
                    out=rest[:], in_=square_sums[:, i, :-1], axis=AX.X, op=ALU.add
                )
                return rest

            def invert_norm(i, rest):
                nc.vector.tensor_scalar(
                    out=norm_sq[:, i : i + 1],
                    in0=square_sums[:, i, square_sums.shape[2] - 1 :],
                    scalar1=rest[:],
                    scalar2=NORM_FLOOR * NORM_FLOOR,
                    op0=ALU.add,
                    op1=ALU.max,
                )
                nc.gpsimd.tensor_tensor(
                    out=inv_norm[:, i : i + 1],
                    in0=norm_sq[:, i : i + 1],
                    in1=minus_half[:],
                    op=ALU.pow,
                )

            def normalise(i, c, on_scalar=False):
                cols = slice(K_PASS * c, K_PASS * (c + 1))
                if on_scalar:
                    nc.scalar.activation(
                        out=unit[i][:, cols],
                        in_=biased[i][:, cols],
                        func=ACT.Copy,
                        scale=inv_norm[:, i : i + 1],
                    )
                else:
                    nc.vector.tensor_scalar_mul(
                        out=unit[i][:, cols], in0=biased[i][:, cols], scalar1=inv_norm[:, i : i + 1]
                    )

            def flip(i, passes, number):
                count = passes.stop - passes.start
                bank = bank_tile(number)
                flipped = bank[:, : 2 * L * count].rearrange("p (c u r) -> p c u r", c=count, u=2)
                words = unit[i][:].bitcast(F32)
                for c in range(count):
                    for u in range(PACK // 2):
                        first_word = K_PASS // 2 * (passes.start + c) + P * u
                        nc.tensor.transpose(
                            flipped[:, c, u, :],
                            words[:, first_word : first_word + P],
                            identity_words[:],
                        )
                nc.scalar.copy(
                    out=grouped_words[:, i, passes], in_=flipped.rearrange("p c u r -> p c r u")
                )

            def quantise(i, passes):
                nc.vector.quantize_mx(
                    out=unit_codes[:, i, passes].rearrange("p c r -> p (c r)").bitcast(FP8X4),
                    scales=unit_planes[:, i, passes].rearrange("p c r -> p (c r)"),
                    in_=grouped_words[:, i, passes]
                    .rearrange("p c r u -> p (c r u)")
                    .bitcast(BF16),
                )

            scores = []

            def score(which, c):
                nc.tensor.matmul_mx(
                    out=scores[which],
                    lhsT=unit_codes[:, 1 - which, c].bitcast(FP8X4),
                    lhsT_scale=unit_planes[:, 1 - which, c],
                    rhs=unit_codes[:, which, c].bitcast(FP8X4),
                    rhs_scale=unit_planes[:, which, c],
                    start=(c == 0),
                    stop=(c == E_PASSES - 1),
                )

            weight = small.tile([P, 2, L], F32)
            shift = small.tile([P, 2], F32)
            row_sum = small.tile([P, 2], F32)
            inv_sum = small.tile([P, 2], F32)

            def find_shifts():
                for which in range(2):
                    negated = small.tile([P, L], F32)
                    nc.vector.tensor_scalar(
                        out=negated[:],
                        in0=scores[which],
                        scalar1=-LAMBDA_ATTN,
                        scalar2=None,
                        op0=ALU.mult,
                        op1=ALU.min,
                        accum_out=shift[:, which : which + 1],
                    )

            def exponentiate():
                for which in range(2):
                    nc.scalar.activation(
                        out=weight[:, which, :],
                        in_=scores[which],
                        func=ACT.Exp,
                        bias=shift[:, which : which + 1],
                        scale=LAMBDA_ATTN,
                        accum_out=row_sum[:, which : which + 1],
                    )

            def invert_sums():
                for which in range(2):
                    nc.vector.reciprocal(
                        out=inv_sum[:, which : which + 1], in_=row_sum[:, which : which + 1]
                    )

            def add_up(which, number):
                summed = bank_tile(number)
                nc.tensor.matmul(
                    summed[:, :L],
                    lhsT=inv_sum[:, which : which + 1].to_broadcast([P, P]),
                    rhs=weight[:, which, :],
                    start=True,
                    stop=True,
                )
                return summed[:, :L]

            return {
                "add_early_squares": add_early_squares,
                "invert_norm": invert_norm,
                "normalise": normalise,
                "flip": flip,
                "quantise": quantise,
                "scores": scores,
                "score": score,
                "find_shifts": find_shifts,
                "exponentiate": exponentiate,
                "invert_sums": invert_sums,
                "add_up": add_up,
            }

        halves = (slice(0, E_PASSES // 2), slice(E_PASSES // 2, E_PASSES))

        def steps_among_passes(stage):
            def flip_image(i):
                for passes, number in zip(halves, SIDE_BANKS):
                    stage["flip"](i, passes, number)

            def quantise_image(i):
                for passes in halves:
                    stage["quantise"](i, passes)

            def step_two():
                quantise_image(0)
                flip_image(1)

            return [lambda: flip_image(0), step_two, lambda: quantise_image(1)]

        def project(i, g, start_col, piece_cols, total):
            s, j = divmod(D_PASSES * head + g, PLANES)
            nc.tensor.matmul_mx(
                out=total[:, :piece_cols],
                lhsT=img_codes[:, i, g, :].bitcast(FP8X4),
                lhsT_scale=img_planes[:, i, g, :],
                rhs=w_codes[:, g, start_col : start_col + piece_cols].bitcast(FP8X4),
                rhs_scale=w_planes[s][
                    4 * j : P, first_col + start_col : first_col + start_col + piece_cols
                ],
                start=(g == 0),
                stop=(g == D_PASSES - 1),
            )

        def add_bias(i, start_col, piece_cols, total, sum_column):
            piece = slice(first_col + start_col, first_col + start_col + piece_cols)
            nc.vector.tensor_tensor(
                out=biased[i][:, piece],
                in0=total[:, :piece_cols],
                in1=bias_all[:, E * head + piece.start : E * head + piece.stop],
                op=ALU.add,
            )
            nc.scalar.activation(
                out=squares[:, :piece_cols],
                in_=biased[i][:, piece],
                func=ACT.Square,
                accum_out=square_sums[:, i, sum_column : sum_column + 1],
            )

        steps = []
        for number, (head, first_col, cols, banks) in enumerate(ROUNDS[:-1]):
            w_codes = loaded[number]
            blocks = cols // BANK
            if first_col == 0:
                biased = [work.tile([P, E], F32, name="biased%d" % i) for i in range(IMAGES)]
                sum_columns = E // BANK + (LAST_PIECES - 1 if head == H - 1 else 0)
                square_sums = small.tile([P, IMAGES, sum_columns], F32, name="squares%d" % head)
                written = 0
                next_step_at = FIRST_STEP_AT
            sums = [
                [bank_tile(banks[blocks * i + c]) for c in range(blocks)] for i in range(IMAGES)
            ]
            for g in range(D_PASSES):
                for i in range(IMAGES):
                    for c in range(blocks):
                        project(i, g, BANK * c, BANK, sums[i][c])
                written += cols
                if steps and written >= next_step_at and g < D_PASSES - 1:
                    steps.pop(0)()
                    next_step_at += STEP_SPACING

            def add_block_bias(i, c):
                add_bias(i, BANK * c, BANK, sums[i][c], first_col // BANK + c)

            if head == 0:
                first_stage = stage = second_stage(head, biased, square_sums)
                for c in range(blocks):
                    add_block_bias(0, c)
                rest = stage["add_early_squares"](0)
                add_block_bias(1, 0)
                stage["invert_norm"](0, rest)
                for c in range(1, blocks):
                    add_block_bias(1, c)
                for c in range(E_PASSES):
                    stage["normalise"](0, c)
                stage["invert_norm"](1, stage["add_early_squares"](1))
                for c in range(E_PASSES):
                    stage["normalise"](1, c)
                steps = steps_among_passes(stage)
            else:
                for i in range(IMAGES):
                    for c in range(blocks):
                        add_block_bias(i, c)

        head, first_col, cols, banks = ROUNDS[-1]
        w_codes = loaded[-1]
        stage = second_stage(head, biased, square_sums)
        last_sums = [[bank_tile(LAST_PIECES * i + c) for c in range(LAST_PIECES)] for i in range(IMAGES)]
        for passes in (range(D_PASSES // 2), range(D_PASSES // 2, D_PASSES)):
            if passes.start == 0:
                order = [(i, g, c) for g in passes for i in range(IMAGES) for c in range(LAST_PIECES)]
            else:
                order = [(i, g, c) for i in range(IMAGES) for c in range(LAST_PIECES) for g in passes]
            for i, g, c in order:
                project(i, g, LAST_PIECE_COLS * c, LAST_PIECE_COLS, last_sums[i][c])

        first_scores = bank_tile(6)
        for which in range(2):
            first_stage["scores"].append(first_scores[:, L * which : L * (which + 1)])
            for c in range(E_PASSES):
                first_stage["score"](which, c)

        def add_last_bias(i, c):
            add_bias(
                i, LAST_PIECE_COLS * c, LAST_PIECE_COLS, last_sums[i][c], first_col // BANK + c
            )

        for c in range(LAST_PIECES):
            add_last_bias(0, c)
        stage["invert_norm"](0, stage["add_early_squares"](0))
        for c in range(LAST_PIECES):
            add_last_bias(1, c)
        rest = stage["add_early_squares"](1)
        for c in range(E_PASSES // 2):
            stage["normalise"](0, c)
        stage["invert_norm"](1, rest)
        first_stage["find_shifts"]()
        stage["normalise"](0, 2)
        stage["normalise"](0, 3, on_scalar=True)
        for c in range(E_PASSES):
            stage["flip"](0, slice(c, c + 1), (4, 5, 7, 0)[c])
        for passes in halves:
            for c in range(passes.start, passes.stop):
                stage["normalise"](1, c)
                stage["flip"](1, slice(c, c + 1), (1, 2, 4, 5)[c])
            stage["quantise"](0, passes)
        first_stage["exponentiate"]()
        for number in (3, 7):
            scores = bank_tile(number)
            stage["scores"].append(scores[:, :L])
        for c in range(E_PASSES):
            stage["quantise"](1, slice(c, c + 1))
            for which in range(2):
                stage["score"](which, c)
        first_stage["invert_sums"]()
        stage["find_shifts"]()
        stage["exponentiate"]()
        stage["invert_sums"]()

        for which, number in zip(range(2), (0, 1)):
            total = first_stage["add_up"](which, number)
            nc.scalar.activation(
                out=result[:, which, 0, :], in_=total, func=ACT.Copy, scale=1.0 / (L + 1e-8)
            )
        for which, number in zip(range(2), (2, 4)):
            total = stage["add_up"](which, number)
            nc.vector.tensor_scalar_mul(
                out=result[:, which, 1, :], in0=total, scalar1=1.0 / (L + 1e-8)
            )

        nc.sync.dma_start(
            out=out.flatten_outer_dims().rearrange("(o s) l -> o (s l)", o=1),
            in_=result[0:1].rearrange("o w h l -> o (w h l)"),
        )
